import numpy as np
import ml_dtypes


def mxq(x, axis, fmt="e4m3"):
    dtype, down = {"e4m3": (ml_dtypes.float8_e4m3fn, 7), "e5m2": (ml_dtypes.float8_e5m2, 14)}[fmt]
    v = np.moveaxis(np.asarray(x, np.float32).astype(ml_dtypes.bfloat16).astype(np.float64), axis, -1)
    blocks = v.reshape(v.shape[:-1] + (-1, 32))
    amax = np.abs(blocks).max(-1, keepdims=True)
    byte = np.maximum(np.where(amax > 0, np.frexp(amax)[1] - 1 + 127, 0) - down, 1)
    scale = np.exp2(byte - 127.0)
    codes = (blocks / scale).astype(np.float32).astype(dtype).astype(np.float64)
    return np.moveaxis((codes * scale).reshape(v.shape), -1, axis)


WIDE = False


def mx_kscale(k):
    if not WIDE:
        return np.ones(k)
    levels = np.array([10, -10, 5, -5, 0])
    a = np.random.permutation(np.resize(levels, k // 512 * 4)).reshape(k // 512, 4)
    idx = np.arange(k)
    return np.exp2(a[idx // 512, idx % 128 // 32])


BF16 = ml_dtypes.bfloat16


def bf(x):
    return np.asarray(x, np.float32).astype(BF16)


def f64(x):
    return np.asarray(x).astype(np.float64)


E2M1 = np.array([0.0, 0.5, 1.0, 1.5, 2.0, 3.0, 4.0, 6.0, -0.0, -0.5, -1.0, -1.5, -2.0, -3.0, -4.0, -6.0])


def pack_weight(w, fmt):
    k, n = w.shape
    w = f64(bf(w)).reshape(k // 32, 32, n)
    amax = np.abs(w).max(1)
    if fmt == "e4m3":
        byte = np.frexp(amax)[1] - 1 + 127 - 7
    else:
        mant, ex = np.frexp(amax / 6.0)
        byte = np.where(mant > 0.5, ex, ex - 1) + 127
    byte = np.clip(np.where(amax > 0, byte, 1), 1, 254)
    scaled = (w * np.exp2(127.0 - byte)[:, None, :]).reshape(k, n).astype(np.float32)
    by_word = np.ascontiguousarray(scaled.reshape(k // 512, 128, 4, n).transpose(0, 1, 3, 2))
    if fmt == "e4m3":
        words = by_word.astype(ml_dtypes.float8_e4m3fn).view(np.uint8)
    else:
        c = by_word.astype(ml_dtypes.float4_e2m1fn).view(np.uint8) & 0xF
        words = c[..., 0::2] | (c[..., 1::2] << 4)
    return np.ascontiguousarray(words), np.ascontiguousarray(byte.astype(np.uint8).reshape(k // 512, 16, n))


def unpack_weight(words, scales, fmt):
    g, p, n, _ = words.shape
    if fmt == "e4m3":
        vals = np.ascontiguousarray(words).view(ml_dtypes.float8_e4m3fn).astype(np.float64)
    else:
        nib = np.empty((g, p, n, 4), np.uint8)
        nib[..., 0::2] = words & 0xF
        nib[..., 1::2] = words >> 4
        vals = E2M1[nib]
    vals = vals * np.repeat(np.exp2(scales.astype(np.float64) - 127.0), 8, axis=1)[..., None]
    return vals.transpose(0, 1, 3, 2).reshape(g * 512, n)


B, G, M, S, H = 256, 10, 4, 512, 512
ALPHA = 1.1


def entmax(alpha, v):
    v = v - np.max(v, axis=-1, keepdims=True)
    e = np.exp(v)
    s = (np.sum(e ** alpha, axis=-1, keepdims=True) + 1e-5) ** (1.0 / alpha)
    return e / s


def layernorm(h, w, b):
    mu = np.mean(h, axis=-1, keepdims=True)
    var = np.mean((h - mu) ** 2, axis=-1, keepdims=True)
    return (h - mu) * (1.0 / np.sqrt(var + 1e-5)) * w + b


def sigmoid(v):
    return 1.0 / (1.0 + np.exp(-v))


def group_matmul(a, w):
    nb, ng, nm, ns = a.shape
    y = a.transpose(1, 0, 2, 3).reshape(ng, nb * nm, ns) @ w.transpose(0, 2, 1)
    return y.reshape(ng, nb, nm, w.shape[1]).transpose(1, 0, 2, 3)


def setup_inputs():
    k = mx_kscale(S)
    ws = 0.003 * S ** (1.0 / ALPHA - 0.5)
    x = bf(np.random.standard_normal((B, G * S)) * np.tile(k, G))
    W_masks = bf(np.random.standard_normal((G, M, S)))
    W1 = (np.random.standard_normal((G, H, S)) + 0.3) * ws / k
    W2 = (np.random.standard_normal((G, H, S)) + 0.3) * ws / k
    W1_words, W1_scales = pack_weight(W1.swapaxes(1, 2).reshape(-1, H), "e4m3")
    W2_words, W2_scales = pack_weight(W2.swapaxes(1, 2).reshape(-1, H), "e4m3")
    return {"x": x,
            "W_masks": W_masks,
            "W1_words": W1_words,
            "W1_scales": W1_scales,
            "W2_words": W2_words,
            "W2_scales": W2_scales,
            "ln1_w": bf(1.0 + 0.2 * np.random.standard_normal((G, H))),
            "ln1_b": bf(0.2 * np.random.standard_normal((G, H))),
            "ln2_w": bf(1.0 + 0.2 * np.random.standard_normal((G, H))),
            "ln2_b": bf(0.2 * np.random.standard_normal((G, H)))}


def reference(x, W_masks, W1_words, W1_scales, W2_words, W2_scales, ln1_w, ln1_b, ln2_w, ln2_b):
    g, m, s = W_masks.shape
    b = x.shape[0]
    xg = f64(x).reshape(b, g, s)
    mask = entmax(ALPHA, f64(W_masks))
    weighted = xg[:, :, None, :] * mask[None]
    wq = mxq(weighted, 3, "e4m3")
    h1 = group_matmul(wq, unpack_weight(W1_words, W1_scales, "e4m3").reshape(G, S, H).swapaxes(1, 2))
    h2 = group_matmul(wq, unpack_weight(W2_words, W2_scales, "e4m3").reshape(G, S, H).swapaxes(1, 2))
    n1 = layernorm(h1, f64(ln1_w)[None, :, None, :], f64(ln1_b)[None, :, None, :])
    n2 = layernorm(h2, f64(ln2_w)[None, :, None, :], f64(ln2_b)[None, :, None, :])
    activated = np.maximum(sigmoid(n1) * n2, 0.0)
    group_out = np.sum(activated, axis=2)
    return group_out.reshape(b, g * group_out.shape[-1])

@@ -1,0 +1,323 @@
+from contextlib import ExitStack
+
+import concourse.mybir as mybir
+from concourse.masks import make_identity
+
+F32 = mybir.dt.float32
+BF16 = mybir.dt.bfloat16
+I32 = mybir.dt.int32
+U32 = mybir.dt.uint32
+U8 = mybir.dt.uint8
+FP8X4 = mybir.dt.float8_e4m3fn_x4
+ALU = mybir.AluOpType
+ACT = mybir.ActivationFunctionType
+AXIS = mybir.AxisListType
+
+P = 128
+PACK = 4
+BATCH = 256
+HALVES = BATCH // P
+GROUPS = 10
+MASKS = 4
+FEATURES = 512
+OUTPUTS = 512
+CHUNKS = OUTPUTS // P
+ALPHA = 1.1
+ENTMAX_EPS = 1e-5
+LN_EPS = 1e-5
+X_LOAD_GROUPS = 2
+UNITS = GROUPS * HALVES
+PAIRS = UNITS * MASKS
+PAIRS_PER_GROUP = HALVES * MASKS
+
+X_AHEAD = 5
+WEIGH_AHEAD = 3
+QUANTISE_AHEAD = 2
+NORMALISE_BEHIND = 2
+ACTIVATE_BEHIND = 6
+MULTIPLY_BEHIND = 7
+ADD_MASKS_BEHIND = 8
+
+FLOPS = 2 * 2 * BATCH * GROUPS * MASKS * FEATURES * OUTPUTS
+
+
+def tile_dynamicfeaturegroupinglayer_e_kernel(
+    tc, x, W_masks, W1_words, W1_scales, W2_words, W2_scales, ln1_w, ln1_b, ln2_w, ln2_b, out
+):
+    nc = tc.nc
+    weight_words = (W1_words, W2_words)
+    weight_scales = (W1_scales, W2_scales)
+    mask_rows = GROUPS * MASKS
+    ln_rows = GROUPS * CHUNKS
+
+    with ExitStack() as ctx:
+        keep = ctx.enter_context(tc.tile_pool(name="keep", bufs=1))
+        x_pool = ctx.enter_context(tc.tile_pool(name="x_pool", bufs=2))
+        quant = ctx.enter_context(tc.tile_pool(name="quant", bufs=6))
+        small = ctx.enter_context(tc.tile_pool(name="small", bufs=6))
+        norm_pool = ctx.enter_context(tc.tile_pool(name="norm_pool", bufs=3))
+        act_pool = ctx.enter_context(tc.tile_pool(name="act_pool", bufs=3))
+        out_pool = ctx.enter_context(tc.tile_pool(name="out_pool", bufs=2))
+        psum_h = ctx.enter_context(tc.psum_pool(name="psum_h", bufs=6))
+        psum_t = ctx.enter_context(tc.psum_pool(name="psum_t", bufs=2))
+
+        logits = keep.tile([P, FEATURES], BF16)
+        ln_raw = keep.tile([P, 4, P], BF16)
+        w_planes = keep.tile([P, 2, GROUPS, OUTPUTS], U8, align_bytes=64)
+        w_words = keep.tile([P, 2, GROUPS, OUTPUTS], U32, align_bytes=64)
+        x_rows = [keep.tile([P, GROUPS * FEATURES], BF16, name="x_rows%d" % h) for h in range(HALVES)]
+        minus_half = keep.tile([P, 2], F32)
+        identity = keep.tile([P, P], F32)
+
+        nc.vector.memset(logits[:], 0.0)
+        nc.vector.memset(w_planes[:].bitcast(I32), 0)
+        nc.vector.memset(ln_raw[:], 0.0)
+        nc.vector.memset(minus_half[:], -0.5)
+        make_identity(nc, identity[:])
+
+        def load_x(first_group):
+            cols = slice(first_group * FEATURES, (first_group + X_LOAD_GROUPS) * FEATURES)
+            for h in range(HALVES):
+                nc.sync.dma_start(out=x_rows[h][:, cols], in_=x[h * P : (h + 1) * P, cols])
+
+        def load_weight_words(g):
+            for w in range(2):
+                nc.sync.dma_start(
+                    out=w_words[:, w, g, :].bitcast(I32),
+                    in_=weight_words[w][g].rearrange("p n t -> p (n t)").bitcast(I32),
+                )
+
+        nc.sync.dma_start(out=logits[0:mask_rows, :], in_=W_masks.rearrange("g m s -> (g m) s"))
+        load_x(0)
+        for w in range(2):
+            for quadrant in range(4):
+                nc.sync.dma_start(
+                    out=w_planes[32 * quadrant : 32 * quadrant + 4, w, :, :].bitcast(I32),
+                    in_=weight_scales[w][:, 4 * quadrant : 4 * quadrant + 4, :]
+                    .rearrange("g r n -> r g n")
+                    .bitcast(I32),
+                )
+        load_weight_words(0)
+        for i, vector in enumerate((ln1_w, ln1_b, ln2_w, ln2_b)):
+            nc.sync.dma_start(
+                out=ln_raw[0:ln_rows, i, :], in_=vector.rearrange("g (c j) -> (g c) j", j=P)
+            )
+        for g in range(1, GROUPS):
+            if g % X_LOAD_GROUPS == 0:
+                load_x(g)
+            load_weight_words(g)
+
+        top = keep.tile([P, 1], F32)
+        nc.vector.reduce_max(out=top[:], in_=logits[:], axis=AXIS.X)
+        minus_alpha_top = keep.tile([P, 1], F32)
+        nc.vector.tensor_scalar_mul(out=minus_alpha_top[:], in0=top[:], scalar1=-ALPHA)
+        powered = keep.tile([P, FEATURES], F32)
+        total = keep.tile([P, 1], F32)
+        nc.scalar.activation(
+            out=powered[:], in_=logits[:], func=ACT.Exp,
+            bias=minus_alpha_top[:], scale=ALPHA, accum_out=total[:],
+        )
+        total_eps = keep.tile([P, 1], F32)
+        nc.vector.tensor_scalar_add(out=total_eps[:], in0=total[:], scalar1=ENTMAX_EPS)
+        log_total = keep.tile([P, 1], F32)
+        nc.scalar.activation(out=log_total[:], in_=total_eps[:], func=ACT.Ln)
+        shift = keep.tile([P, 1], F32)
+        nc.vector.scalar_tensor_tensor(
+            out=shift[:], in0=log_total[:], scalar=-1.0 / ALPHA, in1=top[:],
+            op0=ALU.mult, op1=ALU.subtract,
+        )
+        mask_rows_tp = keep.tile([P, PACK, P], F32)
+        nc.scalar.activation(
+            out=mask_rows_tp[:], in_=logits[:].rearrange("r (p t) -> r t p", t=PACK),
+            func=ACT.Exp, bias=shift[:], scale=1.0,
+        )
+        mask_ps = psum_t.tile([P, PACK, P], F32, tag="t")
+        for t in range(PACK):
+            nc.tensor.transpose(out=mask_ps[:, t, :], in_=mask_rows_tp[:, t, :], identity=identity[:])
+        mask_pt = keep.tile([P, mask_rows, PACK], F32)
+        nc.vector.tensor_copy(
+            out=mask_pt[:], in_=mask_ps[:, :, 0:mask_rows].rearrange("p t r -> p r t")
+        )
+
+        ln_f32 = keep.tile([P, 4, P], F32)
+        nc.vector.tensor_copy(out=ln_f32[:], in_=ln_raw[:])
+        ln_ps = psum_t.tile([P, 4, P], F32, tag="t")
+        for i in range(4):
+            nc.tensor.transpose(out=ln_ps[:, i, :], in_=ln_f32[:, i, :], identity=identity[:])
+        ln_j = keep.tile([P, 4, ln_rows], F32)
+        nc.vector.tensor_copy(out=ln_j[:], in_=ln_ps[:, :, 0:ln_rows])
+
+        x_pt = {}
+        weighted = {}
+        a_words = {}
+        a_planes = {}
+        products = {}
+        stats = {}
+        rstd = {}
+        minus_mean_rstd = {}
+        normed = {}
+        gate = {}
+        value = {}
+
+        def transpose_x(g):
+            x_ps = psum_h.tile([P, HALVES, 2, P], F32, tag="h")
+            for h in range(HALVES):
+                words_of_x = x_rows[h][:].bitcast(F32)
+                for u in range(2):
+                    nc.tensor.transpose(
+                        out=x_ps[:, h, u, :],
+                        in_=words_of_x[:, g * FEATURES // 2 + u : (g + 1) * FEATURES // 2 : 2],
+                        identity=identity[:],
+                    )
+            x_group = x_pool.tile([P, HALVES, P, PACK], BF16)
+            nc.scalar.copy(out=x_group[:].bitcast(F32), in_=x_ps[:].rearrange("p h u b -> p h b u"))
+            x_pt[g] = x_group
+
+        def weigh(k):
+            g, h, m = k // PAIRS_PER_GROUP, k // MASKS % HALVES, k % MASKS
+            rounded = quant.tile([P, P, PACK], BF16, align_bytes=64)
+            nc.vector.tensor_tensor(
+                out=rounded[:],
+                in0=x_pt[g][:, h],
+                in1=mask_pt[:, MASKS * g + m, :].unsqueeze(1).to_broadcast([P, P, PACK]),
+                op=ALU.mult,
+            )
+            weighted[k] = rounded
+
+        def quantise(k):
+            words = quant.tile([P, P], U32, align_bytes=64)
+            planes = quant.tile([P, P], U8, align_bytes=64)
+            nc.vector.quantize_mx(
+                out=words[:].bitcast(FP8X4),
+                scales=planes[:],
+                in_=weighted[k][:].rearrange("p b t -> p (b t)"),
+            )
+            a_words[k] = words
+            a_planes[k] = planes
+
+        def project(k):
+            g = k // PAIRS_PER_GROUP
+            products[k] = []
+            for w in range(2):
+                h_ps = psum_h.tile([P, OUTPUTS], F32, tag="h")
+                nc.tensor.matmul_mx(
+                    out=h_ps[:],
+                    lhsT=a_words[k][:].bitcast(FP8X4),
+                    lhsT_scale=a_planes[k][:],
+                    rhs=w_words[:, w, g, :].bitcast(FP8X4),
+                    rhs_scale=w_planes[:, w, g, :],
+                    start=True,
+                    stop=True,
+                )
+                products[k].append(h_ps)
+            six = small.tile([P, 2, 6], F32)
+            stats[k] = six
+
+        def measure(k, w):
+            nc.vector.bn_stats(out=stats[k][:, w, :], in_=products[k][w][:])
+
+        def scale_and_bias(k):
+            mean_var = small.tile([P, 2, 2], F32)
+            for w in range(2):
+                nc.vector.bn_aggr(out=mean_var[:, w, :], in_=stats[k][:, w, :])
+            var_eps = small.tile([P, 2], F32)
+            nc.gpsimd.tensor_scalar(
+                out=var_eps[:], in0=mean_var[:, :, 1], scalar1=1.0, scalar2=LN_EPS,
+                op0=ALU.mult, op1=ALU.add,
+            )
+            scale = small.tile([P, 2], F32)
+            nc.gpsimd.tensor_tensor(out=scale[:], in0=var_eps[:], in1=minus_half[:], op=ALU.pow)
+            minus_mean = small.tile([P, 2], F32)
+            nc.gpsimd.tensor_scalar(
+                out=minus_mean[:], in0=mean_var[:, :, 0], scalar1=-1.0, scalar2=0.0,
+                op0=ALU.mult, op1=ALU.add,
+            )
+            bias = small.tile([P, 2], F32)
+            nc.gpsimd.tensor_tensor(out=bias[:], in0=minus_mean[:], in1=scale[:], op=ALU.mult)
+            rstd[k] = scale
+            minus_mean_rstd[k] = bias
+
+        def normalise(k):
+            u, m = k // MASKS, k % MASKS
+            if m == 0:
+                unit_normed = norm_pool.tile([P, 2, MASKS, OUTPUTS], F32)
+                normed[u] = unit_normed
+            for w in range(2):
+                nc.scalar.activation(
+                    out=normed[u][:, w, m, :], in_=products[k][w][:], func=ACT.Identity,
+                    scale=rstd[k][:, w : w + 1], bias=minus_mean_rstd[k][:, w : w + 1],
+                )
+
+        def activate(q):
+            u, c = q // CHUNKS, q % CHUNKS
+            if c == 0:
+                unit_gate = act_pool.tile([P, CHUNKS, MASKS * P], F32)
+                unit_value = act_pool.tile([P, CHUNKS, MASKS * P], F32)
+                gate[u] = unit_gate
+                value[u] = unit_value
+            row = CHUNKS * (u // HALVES) + c
+            for w, (func, result) in enumerate(((ACT.Sigmoid, gate[u]), (ACT.Relu, value[u]))):
+                normed_ps = psum_t.tile([P, MASKS, P], F32, tag="t")
+                for m in range(MASKS):
+                    nc.tensor.transpose(
+                        out=normed_ps[:, m, :],
+                        in_=normed[u][:, w, m, c * P : (c + 1) * P],
+                        identity=identity[:],
+                    )
+                nc.scalar.activation(
+                    out=result[:, c, :], in_=normed_ps[:].rearrange("j m b -> j (m b)"), func=func,
+                    scale=ln_j[:, 2 * w, row : row + 1], bias=ln_j[:, 2 * w + 1, row : row + 1],
+                )
+
+        def multiply(q):
+            u, c = q // CHUNKS, q % CHUNKS
+            nc.vector.tensor_tensor(
+                out=value[u][:, c, :], in0=value[u][:, c, :], in1=gate[u][:, c, :], op=ALU.mult
+            )
+
+        def add_masks_and_store(u):
+            g, h = u // HALVES, u % HALVES
+            out_ps = psum_h.tile([P, OUTPUTS], F32, tag="h")
+            for c in range(CHUNKS):
+                for m in range(MASKS):
+                    nc.tensor.matmul(
+                        out=out_ps[:, c * P : (c + 1) * P],
+                        lhsT=value[u][:, c, m * P : (m + 1) * P],
+                        rhs=identity[:],
+                        is_transpose=True,
+                        start=(m == 0),
+                        stop=(m == MASKS - 1),
+                    )
+            out_rows = out_pool.tile([P, OUTPUTS], F32)
+            nc.scalar.copy(out=out_rows[:], in_=out_ps[:])
+            nc.sync.dma_start(
+                out=out[h * P : (h + 1) * P, g * OUTPUTS : (g + 1) * OUTPUTS], in_=out_rows[:]
+            )
+
+        def in_range(index, count):
+            return 0 <= index < count
+
+        with tc.manual_schedule():
+            for k in range(-X_AHEAD, PAIRS + ADD_MASKS_BEHIND + 1):
+                if in_range(k, PAIRS):
+                    project(k)
+                if in_range(k - MULTIPLY_BEHIND, PAIRS):
+                    multiply(k - MULTIPLY_BEHIND)
+                if in_range(k, PAIRS):
+                    measure(k, 0)
+                if in_range(k + WEIGH_AHEAD, PAIRS):
+                    weigh(k + WEIGH_AHEAD)
+                if in_range(k, PAIRS):
+                    measure(k, 1)
+                if in_range(k + QUANTISE_AHEAD, PAIRS):
+                    quantise(k + QUANTISE_AHEAD)
+                if in_range(k, PAIRS):
+                    scale_and_bias(k)
+                if in_range(k - NORMALISE_BEHIND, PAIRS):
+                    normalise(k - NORMALISE_BEHIND)
+                if in_range(k - ACTIVATE_BEHIND, PAIRS):
+                    activate(k - ACTIVATE_BEHIND)
+                if in_range(k - ADD_MASKS_BEHIND, PAIRS) and (k - ADD_MASKS_BEHIND) % CHUNKS == CHUNKS - 1:
+                    add_masks_and_store((k - ADD_MASKS_BEHIND) // CHUNKS)
+                if in_range(k + X_AHEAD, PAIRS) and (k + X_AHEAD) % PAIRS_PER_GROUP == 0:
+                    transpose_x((k + X_AHEAD) // PAIRS_PER_GROUP)

@@ -30,13 +30,15 @@ UNITS = GROUPS * HALVES
 PAIRS = UNITS * MASKS
 PAIRS_PER_GROUP = HALVES * MASKS
 
-X_AHEAD = 5
+X_AHEAD = 7
+X_COPY_AHEAD = 6
 WEIGH_AHEAD = 3
 QUANTISE_AHEAD = 2
-NORMALISE_BEHIND = 2
+NORMALISE_BEHIND = 1
 ACTIVATE_BEHIND = 6
 MULTIPLY_BEHIND = 7
 ADD_MASKS_BEHIND = 8
+STORE_BEHIND = 9
 
 FLOPS = 2 * 2 * BATCH * GROUPS * MASKS * FEATURES * OUTPUTS
 
@@ -147,6 +149,7 @@ def tile_dynamicfeaturegroupinglayer_e_kernel(
         ln_j = keep.tile([P, 4, ln_rows], F32)
         nc.vector.tensor_copy(out=ln_j[:], in_=ln_ps[:, :, 0:ln_rows])
 
+        x_ps = {}
         x_pt = {}
         weighted = {}
         a_words = {}
@@ -158,19 +161,25 @@ def tile_dynamicfeaturegroupinglayer_e_kernel(
         normed = {}
         gate = {}
         value = {}
+        out_ps = {}
 
         def transpose_x(g):
-            x_ps = psum_h.tile([P, HALVES, 2, P], F32, tag="h")
+            words_ps = psum_h.tile([P, HALVES, 2, P], F32, tag="h")
             for h in range(HALVES):
                 words_of_x = x_rows[h][:].bitcast(F32)
                 for u in range(2):
                     nc.tensor.transpose(
-                        out=x_ps[:, h, u, :],
+                        out=words_ps[:, h, u, :],
                         in_=words_of_x[:, g * FEATURES // 2 + u : (g + 1) * FEATURES // 2 : 2],
                         identity=identity[:],
                     )
+            x_ps[g] = words_ps
+
+        def copy_x(g):
             x_group = x_pool.tile([P, HALVES, P, PACK], BF16)
-            nc.scalar.copy(out=x_group[:].bitcast(F32), in_=x_ps[:].rearrange("p h u b -> p h b u"))
+            nc.scalar.copy(
+                out=x_group[:].bitcast(F32), in_=x_ps[g][:].rearrange("p h u b -> p h b u")
+            )
             x_pt[g] = x_group
 
         def weigh(k):
@@ -237,37 +246,37 @@ def tile_dynamicfeaturegroupinglayer_e_kernel(
             rstd[k] = scale
             minus_mean_rstd[k] = bias
 
-        def normalise(k):
+        def normalise(k, w):
             u, m = k // MASKS, k % MASKS
-            if m == 0:
+            if m == 0 and w == 0:
                 unit_normed = norm_pool.tile([P, 2, MASKS, OUTPUTS], F32)
                 normed[u] = unit_normed
-            for w in range(2):
-                nc.scalar.activation(
-                    out=normed[u][:, w, m, :], in_=products[k][w][:], func=ACT.Identity,
-                    scale=rstd[k][:, w : w + 1], bias=minus_mean_rstd[k][:, w : w + 1],
-                )
+            nc.scalar.activation(
+                out=normed[u][:, w, m, :], in_=products[k][w][:], func=ACT.Identity,
+                scale=rstd[k][:, w : w + 1], bias=minus_mean_rstd[k][:, w : w + 1],
+            )
 
-        def activate(q):
+        def activate(q, w):
             u, c = q // CHUNKS, q % CHUNKS
-            if c == 0:
+            if c == 0 and w == 0:
                 unit_gate = act_pool.tile([P, CHUNKS, MASKS * P], F32)
                 unit_value = act_pool.tile([P, CHUNKS, MASKS * P], F32)
                 gate[u] = unit_gate
                 value[u] = unit_value
             row = CHUNKS * (u // HALVES) + c
-            for w, (func, result) in enumerate(((ACT.Sigmoid, gate[u]), (ACT.Relu, value[u]))):
-                normed_ps = psum_t.tile([P, MASKS, P], F32, tag="t")
-                for m in range(MASKS):
-                    nc.tensor.transpose(
-                        out=normed_ps[:, m, :],
-                        in_=normed[u][:, w, m, c * P : (c + 1) * P],
-                        identity=identity[:],
-                    )
-                nc.scalar.activation(
-                    out=result[:, c, :], in_=normed_ps[:].rearrange("j m b -> j (m b)"), func=func,
-                    scale=ln_j[:, 2 * w, row : row + 1], bias=ln_j[:, 2 * w + 1, row : row + 1],
+            normed_ps = psum_t.tile([P, MASKS, P], F32, tag="t")
+            for m in range(MASKS):
+                nc.tensor.transpose(
+                    out=normed_ps[:, m, :],
+                    in_=normed[u][:, w, m, c * P : (c + 1) * P],
+                    identity=identity[:],
                 )
+            nc.scalar.activation(
+                out=(gate[u], value[u])[w][:, c, :],
+                in_=normed_ps[:].rearrange("j m b -> j (m b)"),
+                func=(ACT.Sigmoid, ACT.Relu)[w],
+                scale=ln_j[:, 2 * w, row : row + 1], bias=ln_j[:, 2 * w + 1, row : row + 1],
+            )
 
         def multiply(q):
             u, c = q // CHUNKS, q % CHUNKS
@@ -275,21 +284,24 @@ def tile_dynamicfeaturegroupinglayer_e_kernel(
                 out=value[u][:, c, :], in0=value[u][:, c, :], in1=gate[u][:, c, :], op=ALU.mult
             )
 
-        def add_masks_and_store(u):
-            g, h = u // HALVES, u % HALVES
-            out_ps = psum_h.tile([P, OUTPUTS], F32, tag="h")
+        def add_masks(u):
+            sums_ps = psum_h.tile([P, OUTPUTS], F32, tag="h")
             for c in range(CHUNKS):
                 for m in range(MASKS):
                     nc.tensor.matmul(
-                        out=out_ps[:, c * P : (c + 1) * P],
+                        out=sums_ps[:, c * P : (c + 1) * P],
                         lhsT=value[u][:, c, m * P : (m + 1) * P],
                         rhs=identity[:],
                         is_transpose=True,
                         start=(m == 0),
                         stop=(m == MASKS - 1),
                     )
+            out_ps[u] = sums_ps
+
+        def store(u):
+            g, h = u // HALVES, u % HALVES
             out_rows = out_pool.tile([P, OUTPUTS], F32)
-            nc.scalar.copy(out=out_rows[:], in_=out_ps[:])
+            nc.scalar.copy(out=out_rows[:], in_=out_ps[u][:])
             nc.sync.dma_start(
                 out=out[h * P : (h + 1) * P, g * OUTPUTS : (g + 1) * OUTPUTS], in_=out_rows[:]
             )
@@ -297,27 +309,36 @@ def tile_dynamicfeaturegroupinglayer_e_kernel(
         def in_range(index, count):
             return 0 <= index < count
 
+        def first_of_group(k):
+            return in_range(k, PAIRS) and k % PAIRS_PER_GROUP == 0
+
+        def last_of_unit(q):
+            return in_range(q, PAIRS) and q % CHUNKS == CHUNKS - 1
+
         with tc.manual_schedule():
-            for k in range(-X_AHEAD, PAIRS + ADD_MASKS_BEHIND + 1):
+            for k in range(-X_AHEAD, PAIRS + STORE_BEHIND):
                 if in_range(k, PAIRS):
                     project(k)
-                if in_range(k - MULTIPLY_BEHIND, PAIRS):
-                    multiply(k - MULTIPLY_BEHIND)
-                if in_range(k, PAIRS):
                     measure(k, 0)
-                if in_range(k + WEIGH_AHEAD, PAIRS):
-                    weigh(k + WEIGH_AHEAD)
-                if in_range(k, PAIRS):
                     measure(k, 1)
                 if in_range(k + QUANTISE_AHEAD, PAIRS):
                     quantise(k + QUANTISE_AHEAD)
                 if in_range(k, PAIRS):
                     scale_and_bias(k)
-                if in_range(k - NORMALISE_BEHIND, PAIRS):
-                    normalise(k - NORMALISE_BEHIND)
-                if in_range(k - ACTIVATE_BEHIND, PAIRS):
-                    activate(k - ACTIVATE_BEHIND)
-                if in_range(k - ADD_MASKS_BEHIND, PAIRS) and (k - ADD_MASKS_BEHIND) % CHUNKS == CHUNKS - 1:
-                    add_masks_and_store((k - ADD_MASKS_BEHIND) // CHUNKS)
-                if in_range(k + X_AHEAD, PAIRS) and (k + X_AHEAD) % PAIRS_PER_GROUP == 0:
+                if in_range(k - MULTIPLY_BEHIND, PAIRS):
+                    multiply(k - MULTIPLY_BEHIND)
+                if in_range(k + WEIGH_AHEAD, PAIRS):
+                    weigh(k + WEIGH_AHEAD)
+                for w in range(2):
+                    if in_range(k - ACTIVATE_BEHIND, PAIRS):
+                        activate(k - ACTIVATE_BEHIND, w)
+                    if in_range(k - NORMALISE_BEHIND, PAIRS):
+                        normalise(k - NORMALISE_BEHIND, w)
+                if last_of_unit(k - ADD_MASKS_BEHIND):
+                    add_masks((k - ADD_MASKS_BEHIND) // CHUNKS)
+                if last_of_unit(k - STORE_BEHIND):
+                    store((k - STORE_BEHIND) // CHUNKS)
+                if first_of_group(k + X_AHEAD):
                     transpose_x((k + X_AHEAD) // PAIRS_PER_GROUP)
+                if first_of_group(k + X_COPY_AHEAD):
+                    copy_x((k + X_COPY_AHEAD) // PAIRS_PER_GROUP)

@@ -30,15 +30,16 @@ UNITS = GROUPS * HALVES
 PAIRS = UNITS * MASKS
 PAIRS_PER_GROUP = HALVES * MASKS
 
-X_AHEAD = 7
-X_COPY_AHEAD = 6
+X_AHEAD = 8
+X_COPY_AHEAD = 7
 WEIGH_AHEAD = 3
 QUANTISE_AHEAD = 2
-NORMALISE_BEHIND = 1
-ACTIVATE_BEHIND = 6
-MULTIPLY_BEHIND = 7
-ADD_MASKS_BEHIND = 8
-STORE_BEHIND = 9
+PROJECT_AGAIN_BEHIND = 6
+NORMALISE_BEHIND = 7
+ACTIVATE_BEHIND = 11
+MULTIPLY_BEHIND = 12
+ADD_MASKS_BEHIND = 13
+STORE_BEHIND = 14
 
 FLOPS = 2 * 2 * BATCH * GROUPS * MASKS * FEATURES * OUTPUTS
 
@@ -55,20 +56,25 @@ def tile_dynamicfeaturegroupinglayer_e_kernel(
     with ExitStack() as ctx:
         keep = ctx.enter_context(tc.tile_pool(name="keep", bufs=1))
         x_pool = ctx.enter_context(tc.tile_pool(name="x_pool", bufs=2))
-        quant = ctx.enter_context(tc.tile_pool(name="quant", bufs=6))
-        small = ctx.enter_context(tc.tile_pool(name="small", bufs=6))
+        round_pool = ctx.enter_context(tc.tile_pool(name="round_pool", bufs=3))
+        code_pool = ctx.enter_context(
+            tc.tile_pool(name="code_pool", bufs=QUANTISE_AHEAD + PROJECT_AGAIN_BEHIND + 2)
+        )
+        small = ctx.enter_context(tc.tile_pool(name="small", bufs=4))
         norm_pool = ctx.enter_context(tc.tile_pool(name="norm_pool", bufs=3))
         act_pool = ctx.enter_context(tc.tile_pool(name="act_pool", bufs=3))
         out_pool = ctx.enter_context(tc.tile_pool(name="out_pool", bufs=2))
-        psum_h = ctx.enter_context(tc.psum_pool(name="psum_h", bufs=6))
-        psum_t = ctx.enter_context(tc.psum_pool(name="psum_t", bufs=2))
+        psum_measure = ctx.enter_context(tc.psum_pool(name="psum_measure", bufs=2))
+        psum_normalise = ctx.enter_context(tc.psum_pool(name="psum_normalise", bufs=2))
+        psum_t = ctx.enter_context(tc.psum_pool(name="psum_t", bufs=3))
+        psum_sum = ctx.enter_context(tc.psum_pool(name="psum_sum", bufs=1))
 
         logits = keep.tile([P, FEATURES], BF16)
         ln_raw = keep.tile([P, 4, P], BF16)
         w_planes = keep.tile([P, 2, GROUPS, OUTPUTS], U8, align_bytes=64)
         w_words = keep.tile([P, 2, GROUPS, OUTPUTS], U32, align_bytes=64)
         x_rows = [keep.tile([P, GROUPS * FEATURES], BF16, name="x_rows%d" % h) for h in range(HALVES)]
-        minus_half = keep.tile([P, 2], F32)
+        minus_half = keep.tile([P, 2 * MASKS], F32)
         identity = keep.tile([P, P], F32)
 
         nc.vector.memset(logits[:], 0.0)
@@ -154,17 +160,20 @@ def tile_dynamicfeaturegroupinglayer_e_kernel(
         weighted = {}
         a_words = {}
         a_planes = {}
-        products = {}
+        measured_ps = {}
         stats = {}
+        products = {}
+        mean_var = {}
         rstd = {}
         minus_mean_rstd = {}
         normed = {}
         gate = {}
         value = {}
         out_ps = {}
+        normed_ps = {}
 
         def transpose_x(g):
-            words_ps = psum_h.tile([P, HALVES, 2, P], F32, tag="h")
+            words_ps = psum_t.tile([P, HALVES, 2, P], F32, tag="t")
             for h in range(HALVES):
                 words_of_x = x_rows[h][:].bitcast(F32)
                 for u in range(2):
@@ -184,7 +193,7 @@ def tile_dynamicfeaturegroupinglayer_e_kernel(
 
         def weigh(k):
             g, h, m = k // PAIRS_PER_GROUP, k // MASKS % HALVES, k % MASKS
-            rounded = quant.tile([P, P, PACK], BF16, align_bytes=64)
+            rounded = round_pool.tile([P, P, PACK], BF16, align_bytes=64)
             nc.vector.tensor_tensor(
                 out=rounded[:],
                 in0=x_pt[g][:, h],
@@ -194,8 +203,8 @@ def tile_dynamicfeaturegroupinglayer_e_kernel(
             weighted[k] = rounded
 
         def quantise(k):
-            words = quant.tile([P, P], U32, align_bytes=64)
-            planes = quant.tile([P, P], U8, align_bytes=64)
+            words = code_pool.tile([P, P], U32, align_bytes=64)
+            planes = code_pool.tile([P, P], U8, align_bytes=64)
             nc.vector.quantize_mx(
                 out=words[:].bitcast(FP8X4),
                 scales=planes[:],
@@ -204,11 +213,11 @@ def tile_dynamicfeaturegroupinglayer_e_kernel(
             a_words[k] = words
             a_planes[k] = planes
 
-        def project(k):
+        def project(k, pool):
             g = k // PAIRS_PER_GROUP
-            products[k] = []
+            pair = []
             for w in range(2):
-                h_ps = psum_h.tile([P, OUTPUTS], F32, tag="h")
+                h_ps = pool.tile([P, OUTPUTS], F32, tag="h")
                 nc.tensor.matmul_mx(
                     out=h_ps[:],
                     lhsT=a_words[k][:].bitcast(FP8X4),
@@ -218,65 +227,83 @@ def tile_dynamicfeaturegroupinglayer_e_kernel(
                     start=True,
                     stop=True,
                 )
-                products[k].append(h_ps)
+                pair.append(h_ps)
+            return pair
+
+        def measure(k):
             six = small.tile([P, 2, 6], F32)
+            for w in range(2):
+                nc.vector.bn_stats(out=six[:, w, :], in_=measured_ps[k][w][:])
             stats[k] = six
 
-        def measure(k, w):
-            nc.vector.bn_stats(out=stats[k][:, w, :], in_=products[k][w][:])
-
-        def scale_and_bias(k):
-            mean_var = small.tile([P, 2, 2], F32)
-            for w in range(2):
-                nc.vector.bn_aggr(out=mean_var[:, w, :], in_=stats[k][:, w, :])
-            var_eps = small.tile([P, 2], F32)
-            nc.gpsimd.tensor_scalar(
-                out=var_eps[:], in0=mean_var[:, :, 1], scalar1=1.0, scalar2=LN_EPS,
-                op0=ALU.mult, op1=ALU.add,
-            )
-            scale = small.tile([P, 2], F32)
-            nc.gpsimd.tensor_tensor(out=scale[:], in0=var_eps[:], in1=minus_half[:], op=ALU.pow)
-            minus_mean = small.tile([P, 2], F32)
-            nc.gpsimd.tensor_scalar(
-                out=minus_mean[:], in0=mean_var[:, :, 0], scalar1=-1.0, scalar2=0.0,
-                op0=ALU.mult, op1=ALU.add,
-            )
-            bias = small.tile([P, 2], F32)
-            nc.gpsimd.tensor_tensor(out=bias[:], in0=minus_mean[:], in1=scale[:], op=ALU.mult)
-            rstd[k] = scale
-            minus_mean_rstd[k] = bias
-
-        def normalise(k, w):
+        def aggregate(k):
             u, m = k // MASKS, k % MASKS
-            if m == 0 and w == 0:
+            if m == 0:
+                unit_mean_var = small.tile([P, MASKS, 2, 2], F32)
+                mean_var[u] = unit_mean_var
+            for w in range(2):
+                nc.vector.bn_aggr(out=mean_var[u][:, m, w, :], in_=stats[k][:, w, :])
+
+        def scale_and_bias(u):
+            means = mean_var[u][:].rearrange("p m w s -> p (m w) s")[:, :, 0]
+            variances = mean_var[u][:].rearrange("p m w s -> p (m w) s")[:, :, 1]
+            var_eps = small.tile([P, 2 * MASKS], F32)
+            nc.gpsimd.tensor_scalar(
+                out=var_eps[:], in0=variances, scalar1=1.0, scalar2=LN_EPS,
+                op0=ALU.mult, op1=ALU.add,
+            )
+            scale = small.tile([P, 2 * MASKS], F32)
+            nc.gpsimd.tensor_tensor(out=scale[:], in0=var_eps[:], in1=minus_half[:], op=ALU.pow)
+            minus_mean = small.tile([P, 2 * MASKS], F32)
+            nc.gpsimd.tensor_scalar(
+                out=minus_mean[:], in0=means, scalar1=-1.0, scalar2=0.0,
+                op0=ALU.mult, op1=ALU.add,
+            )
+            bias = small.tile([P, 2 * MASKS], F32)
+            nc.gpsimd.tensor_tensor(out=bias[:], in0=minus_mean[:], in1=scale[:], op=ALU.mult)
+            rstd[u] = scale
+            minus_mean_rstd[u] = bias
+
+        def normalise(k):
+            u, m = k // MASKS, k % MASKS
+            if m == 0:
                 unit_normed = norm_pool.tile([P, 2, MASKS, OUTPUTS], F32)
                 normed[u] = unit_normed
-            nc.scalar.activation(
-                out=normed[u][:, w, m, :], in_=products[k][w][:], func=ACT.Identity,
-                scale=rstd[k][:, w : w + 1], bias=minus_mean_rstd[k][:, w : w + 1],
-            )
+            for w in range(2):
+                column = 2 * m + w
+                nc.scalar.activation(
+                    out=normed[u][:, w, m, :], in_=products[k][w][:], func=ACT.Identity,
+                    scale=rstd[u][:, column : column + 1],
+                    bias=minus_mean_rstd[u][:, column : column + 1],
+                )
 
-        def activate(q, w):
+        def transpose_normed(q):
             u, c = q // CHUNKS, q % CHUNKS
-            if c == 0 and w == 0:
+            normed_ps[q] = []
+            for w in range(2):
+                chunk_ps = psum_t.tile([P, MASKS, P], F32, tag="t")
+                for m in range(MASKS):
+                    nc.tensor.transpose(
+                        out=chunk_ps[:, m, :],
+                        in_=normed[u][:, w, m, c * P : (c + 1) * P],
+                        identity=identity[:],
+                    )
+                normed_ps[q].append(chunk_ps)
+
+        def activate(q):
+            u, c = q // CHUNKS, q % CHUNKS
+            if c == 0:
                 unit_gate = act_pool.tile([P, CHUNKS, MASKS * P], F32)
                 unit_value = act_pool.tile([P, CHUNKS, MASKS * P], F32)
                 gate[u] = unit_gate
                 value[u] = unit_value
             row = CHUNKS * (u // HALVES) + c
-            normed_ps = psum_t.tile([P, MASKS, P], F32, tag="t")
-            for m in range(MASKS):
-                nc.tensor.transpose(
-                    out=normed_ps[:, m, :],
-                    in_=normed[u][:, w, m, c * P : (c + 1) * P],
-                    identity=identity[:],
+            for w, (func, result) in enumerate(((ACT.Sigmoid, gate[u]), (ACT.Relu, value[u]))):
+                nc.scalar.activation(
+                    out=result[:, c, :], in_=normed_ps[q][w][:].rearrange("j m b -> j (m b)"),
+                    func=func,
+                    scale=ln_j[:, 2 * w, row : row + 1], bias=ln_j[:, 2 * w + 1, row : row + 1],
                 )
-            nc.scalar.activation(
-                out=(gate[u], value[u])[w][:, c, :],
-                in_=normed_ps[:].rearrange("j m b -> j (m b)"),
-                func=(ACT.Sigmoid, ACT.Relu)[w],
-                scale=ln_j[:, 2 * w, row : row + 1], bias=ln_j[:, 2 * w + 1, row : row + 1],
-            )
 
         def multiply(q):
             u, c = q // CHUNKS, q % CHUNKS
@@ -284,19 +311,20 @@ def tile_dynamicfeaturegroupinglayer_e_kernel(
                 out=value[u][:, c, :], in0=value[u][:, c, :], in1=gate[u][:, c, :], op=ALU.mult
             )
 
-        def add_masks(u):
-            sums_ps = psum_h.tile([P, OUTPUTS], F32, tag="h")
-            for c in range(CHUNKS):
-                for m in range(MASKS):
-                    nc.tensor.matmul(
-                        out=sums_ps[:, c * P : (c + 1) * P],
-                        lhsT=value[u][:, c, m * P : (m + 1) * P],
-                        rhs=identity[:],
-                        is_transpose=True,
-                        start=(m == 0),
-                        stop=(m == MASKS - 1),
-                    )
-            out_ps[u] = sums_ps
+        def add_masks(q):
+            u, c = q // CHUNKS, q % CHUNKS
+            if c == 0:
+                sums_ps = psum_sum.tile([P, OUTPUTS], F32)
+                out_ps[u] = sums_ps
+            for m in range(MASKS):
+                nc.tensor.matmul(
+                    out=out_ps[u][:, c * P : (c + 1) * P],
+                    lhsT=value[u][:, c, m * P : (m + 1) * P],
+                    rhs=identity[:],
+                    is_transpose=True,
+                    start=(m == 0),
+                    stop=(m == MASKS - 1),
+                )
 
         def store(u):
             g, h = u // HALVES, u % HALVES
@@ -306,39 +334,46 @@ def tile_dynamicfeaturegroupinglayer_e_kernel(
                 out=out[h * P : (h + 1) * P, g * OUTPUTS : (g + 1) * OUTPUTS], in_=out_rows[:]
             )
 
-        def in_range(index, count):
-            return 0 <= index < count
+        def in_range(index):
+            return 0 <= index < PAIRS
 
         def first_of_group(k):
-            return in_range(k, PAIRS) and k % PAIRS_PER_GROUP == 0
+            return in_range(k) and k % PAIRS_PER_GROUP == 0
 
-        def last_of_unit(q):
-            return in_range(q, PAIRS) and q % CHUNKS == CHUNKS - 1
+        def last_of_unit(k):
+            return in_range(k) and k % MASKS == MASKS - 1
 
         with tc.manual_schedule():
             for k in range(-X_AHEAD, PAIRS + STORE_BEHIND):
-                if in_range(k, PAIRS):
-                    project(k)
-                    measure(k, 0)
-                    measure(k, 1)
-                if in_range(k + QUANTISE_AHEAD, PAIRS):
-                    quantise(k + QUANTISE_AHEAD)
-                if in_range(k, PAIRS):
-                    scale_and_bias(k)
-                if in_range(k - MULTIPLY_BEHIND, PAIRS):
-                    multiply(k - MULTIPLY_BEHIND)
-                if in_range(k + WEIGH_AHEAD, PAIRS):
-                    weigh(k + WEIGH_AHEAD)
-                for w in range(2):
-                    if in_range(k - ACTIVATE_BEHIND, PAIRS):
-                        activate(k - ACTIVATE_BEHIND, w)
-                    if in_range(k - NORMALISE_BEHIND, PAIRS):
-                        normalise(k - NORMALISE_BEHIND, w)
-                if last_of_unit(k - ADD_MASKS_BEHIND):
-                    add_masks((k - ADD_MASKS_BEHIND) // CHUNKS)
-                if last_of_unit(k - STORE_BEHIND):
-                    store((k - STORE_BEHIND) // CHUNKS)
+                if in_range(k - ACTIVATE_BEHIND):
+                    transpose_normed(k - ACTIVATE_BEHIND)
+                if in_range(k):
+                    measured_ps[k] = project(k, psum_measure)
+                if in_range(k - PROJECT_AGAIN_BEHIND):
+                    products[k - PROJECT_AGAIN_BEHIND] = project(k - PROJECT_AGAIN_BEHIND, psum_normalise)
+                if in_range(k - ADD_MASKS_BEHIND):
+                    add_masks(k - ADD_MASKS_BEHIND)
                 if first_of_group(k + X_AHEAD):
                     transpose_x((k + X_AHEAD) // PAIRS_PER_GROUP)
+
+                if in_range(k):
+                    measure(k)
+                if in_range(k + QUANTISE_AHEAD):
+                    quantise(k + QUANTISE_AHEAD)
+                if in_range(k):
+                    aggregate(k)
+                if last_of_unit(k):
+                    scale_and_bias(k // MASKS)
+                if in_range(k - MULTIPLY_BEHIND):
+                    multiply(k - MULTIPLY_BEHIND)
+                if in_range(k + WEIGH_AHEAD):
+                    weigh(k + WEIGH_AHEAD)
+
+                if last_of_unit(k - STORE_BEHIND):
+                    store((k - STORE_BEHIND) // MASKS)
+                if in_range(k - NORMALISE_BEHIND):
+                    normalise(k - NORMALISE_BEHIND)
+                if in_range(k - ACTIVATE_BEHIND):
+                    activate(k - ACTIVATE_BEHIND)
                 if first_of_group(k + X_COPY_AHEAD):
                     copy_x((k + X_COPY_AHEAD) // PAIRS_PER_GROUP)

@@ -30,16 +30,15 @@ UNITS = GROUPS * HALVES
 PAIRS = UNITS * MASKS
 PAIRS_PER_GROUP = HALVES * MASKS
 
-X_AHEAD = 8
-X_COPY_AHEAD = 7
-WEIGH_AHEAD = 3
+X_AHEAD = 6
+WEIGH_AHEAD = 5
 QUANTISE_AHEAD = 2
-PROJECT_AGAIN_BEHIND = 6
-NORMALISE_BEHIND = 7
-ACTIVATE_BEHIND = 11
-MULTIPLY_BEHIND = 12
-ADD_MASKS_BEHIND = 13
-STORE_BEHIND = 14
+PROJECT_AGAIN_BEHIND = 5
+NORMALISE_BEHIND = 6
+ACTIVATE_BEHIND = 10
+MULTIPLY_BEHIND = 11
+ADD_MASKS_BEHIND = 14
+STORE_BEHIND = 15
 
 FLOPS = 2 * 2 * BATCH * GROUPS * MASKS * FEATURES * OUTPUTS
 
@@ -55,18 +54,16 @@ def tile_dynamicfeaturegroupinglayer_e_kernel(
 
     with ExitStack() as ctx:
         keep = ctx.enter_context(tc.tile_pool(name="keep", bufs=1))
-        x_pool = ctx.enter_context(tc.tile_pool(name="x_pool", bufs=2))
-        round_pool = ctx.enter_context(tc.tile_pool(name="round_pool", bufs=3))
-        code_pool = ctx.enter_context(
-            tc.tile_pool(name="code_pool", bufs=QUANTISE_AHEAD + PROJECT_AGAIN_BEHIND + 2)
-        )
+        round_pool = ctx.enter_context(tc.tile_pool(name="round_pool", bufs=2))
+        code_pool = ctx.enter_context(tc.tile_pool(name="code_pool", bufs=4))
         small = ctx.enter_context(tc.tile_pool(name="small", bufs=4))
         norm_pool = ctx.enter_context(tc.tile_pool(name="norm_pool", bufs=3))
         act_pool = ctx.enter_context(tc.tile_pool(name="act_pool", bufs=3))
         out_pool = ctx.enter_context(tc.tile_pool(name="out_pool", bufs=2))
+        psum_x = ctx.enter_context(tc.psum_pool(name="psum_x", bufs=1))
         psum_measure = ctx.enter_context(tc.psum_pool(name="psum_measure", bufs=2))
         psum_normalise = ctx.enter_context(tc.psum_pool(name="psum_normalise", bufs=2))
-        psum_t = ctx.enter_context(tc.psum_pool(name="psum_t", bufs=3))
+        psum_t = ctx.enter_context(tc.psum_pool(name="psum_t", bufs=2))
         psum_sum = ctx.enter_context(tc.psum_pool(name="psum_sum", bufs=1))
 
         logits = keep.tile([P, FEATURES], BF16)
@@ -156,13 +153,12 @@ def tile_dynamicfeaturegroupinglayer_e_kernel(
         nc.vector.tensor_copy(out=ln_j[:], in_=ln_ps[:, :, 0:ln_rows])
 
         x_ps = {}
-        x_pt = {}
-        weighted = {}
-        a_words = {}
-        a_planes = {}
         measured_ps = {}
         stats = {}
         products = {}
+        weighted = {}
+        a_words = {}
+        a_planes = {}
         mean_var = {}
         rstd = {}
         minus_mean_rstd = {}
@@ -173,7 +169,7 @@ def tile_dynamicfeaturegroupinglayer_e_kernel(
         normed_ps = {}
 
         def transpose_x(g):
-            words_ps = psum_t.tile([P, HALVES, 2, P], F32, tag="t")
+            words_ps = psum_x.tile([P, HALVES, 2, P], F32)
             for h in range(HALVES):
                 words_of_x = x_rows[h][:].bitcast(F32)
                 for u in range(2):
@@ -184,44 +180,42 @@ def tile_dynamicfeaturegroupinglayer_e_kernel(
                     )
             x_ps[g] = words_ps
 
-        def copy_x(g):
-            x_group = x_pool.tile([P, HALVES, P, PACK], BF16)
-            nc.scalar.copy(
-                out=x_group[:].bitcast(F32), in_=x_ps[g][:].rearrange("p h u b -> p h b u")
-            )
-            x_pt[g] = x_group
-
         def weigh(k):
             g, h, m = k // PAIRS_PER_GROUP, k // MASKS % HALVES, k % MASKS
-            rounded = round_pool.tile([P, P, PACK], BF16, align_bytes=64)
+            if m == 0:
+                rounded = round_pool.tile([P, MASKS, P, PACK], BF16, align_bytes=64)
+                weighted[k // MASKS] = rounded
             nc.vector.tensor_tensor(
-                out=rounded[:],
-                in0=x_pt[g][:, h],
-                in1=mask_pt[:, MASKS * g + m, :].unsqueeze(1).to_broadcast([P, P, PACK]),
+                out=weighted[k // MASKS][:, m].rearrange("p b (u e) -> p b u e", e=2),
+                in0=x_ps[g][:].bitcast(BF16)[:, h].rearrange("p u (b e) -> p b u e", e=2),
+                in1=mask_pt[:, MASKS * g + m, :]
+                .rearrange("p (u e) -> p u e", e=2)
+                .unsqueeze(1)
+                .to_broadcast([P, P, 2, 2]),
                 op=ALU.mult,
             )
-            weighted[k] = rounded
 
-        def quantise(k):
-            words = code_pool.tile([P, P], U32, align_bytes=64)
-            planes = code_pool.tile([P, P], U8, align_bytes=64)
+        def quantise(u):
+            words = code_pool.tile([P, MASKS * P], U32, align_bytes=64)
+            planes = code_pool.tile([P, MASKS * P], U8, align_bytes=64)
             nc.vector.quantize_mx(
                 out=words[:].bitcast(FP8X4),
                 scales=planes[:],
-                in_=weighted[k][:].rearrange("p b t -> p (b t)"),
+                in_=weighted[u][:].rearrange("p m b t -> p (m b t)"),
             )
-            a_words[k] = words
-            a_planes[k] = planes
+            a_words[u] = words
+            a_planes[u] = planes
 
         def project(k, pool):
-            g = k // PAIRS_PER_GROUP
+            g, u, m = k // PAIRS_PER_GROUP, k // MASKS, k % MASKS
+            rows = slice(m * P, (m + 1) * P)
             pair = []
             for w in range(2):
                 h_ps = pool.tile([P, OUTPUTS], F32, tag="h")
                 nc.tensor.matmul_mx(
                     out=h_ps[:],
-                    lhsT=a_words[k][:].bitcast(FP8X4),
-                    lhsT_scale=a_planes[k][:],
+                    lhsT=a_words[u][:, rows].bitcast(FP8X4),
+                    lhsT_scale=a_planes[u][:, rows],
                     rhs=w_words[:, w, g, :].bitcast(FP8X4),
                     rhs_scale=w_planes[:, w, g, :],
                     start=True,
@@ -307,7 +301,7 @@ def tile_dynamicfeaturegroupinglayer_e_kernel(
 
         def multiply(q):
             u, c = q // CHUNKS, q % CHUNKS
-            nc.vector.tensor_tensor(
+            nc.gpsimd.tensor_tensor(
                 out=value[u][:, c, :], in0=value[u][:, c, :], in1=gate[u][:, c, :], op=ALU.mult
             )
 
@@ -329,7 +323,7 @@ def tile_dynamicfeaturegroupinglayer_e_kernel(
         def store(u):
             g, h = u // HALVES, u % HALVES
             out_rows = out_pool.tile([P, OUTPUTS], F32)
-            nc.scalar.copy(out=out_rows[:], in_=out_ps[u][:])
+            nc.vector.tensor_copy(out=out_rows[:], in_=out_ps[u][:])
             nc.sync.dma_start(
                 out=out[h * P : (h + 1) * P, g * OUTPUTS : (g + 1) * OUTPUTS], in_=out_rows[:]
             )
@@ -339,6 +333,9 @@ def tile_dynamicfeaturegroupinglayer_e_kernel(
 
         def first_of_group(k):
             return in_range(k) and k % PAIRS_PER_GROUP == 0
+
+        def first_of_unit(k):
+            return in_range(k) and k % MASKS == 0
 
         def last_of_unit(k):
             return in_range(k) and k % MASKS == MASKS - 1
@@ -356,24 +353,21 @@ def tile_dynamicfeaturegroupinglayer_e_kernel(
                 if first_of_group(k + X_AHEAD):
                     transpose_x((k + X_AHEAD) // PAIRS_PER_GROUP)
 
+                if in_range(k + WEIGH_AHEAD):
+                    weigh(k + WEIGH_AHEAD)
+                if last_of_unit(k - STORE_BEHIND):
+                    store((k - STORE_BEHIND) // MASKS)
                 if in_range(k):
                     measure(k)
-                if in_range(k + QUANTISE_AHEAD):
-                    quantise(k + QUANTISE_AHEAD)
-                if in_range(k):
                     aggregate(k)
                 if last_of_unit(k):
                     scale_and_bias(k // MASKS)
+                if first_of_unit(k + QUANTISE_AHEAD):
+                    quantise((k + QUANTISE_AHEAD) // MASKS)
                 if in_range(k - MULTIPLY_BEHIND):
                     multiply(k - MULTIPLY_BEHIND)
-                if in_range(k + WEIGH_AHEAD):
-                    weigh(k + WEIGH_AHEAD)
 
-                if last_of_unit(k - STORE_BEHIND):
-                    store((k - STORE_BEHIND) // MASKS)
                 if in_range(k - NORMALISE_BEHIND):
                     normalise(k - NORMALISE_BEHIND)
                 if in_range(k - ACTIVATE_BEHIND):
                     activate(k - ACTIVATE_BEHIND)
-                if first_of_group(k + X_COPY_AHEAD):
-                    copy_x((k + X_COPY_AHEAD) // PAIRS_PER_GROUP)

@@ -30,6 +30,7 @@ UNITS = GROUPS * HALVES
 PAIRS = UNITS * MASKS
 PAIRS_PER_GROUP = HALVES * MASKS
 
+LN_VECTORS_STEP = 1
 X_AHEAD = 6
 WEIGH_AHEAD = 5
 QUANTISE_AHEAD = 2
@@ -74,7 +75,12 @@ def tile_dynamicfeaturegroupinglayer_e_kernel(
         minus_half = keep.tile([P, 2 * MASKS], F32)
         identity = keep.tile([P, P], F32)
 
+        warm = keep.tile([P, 1], F32)
+        zero = keep.tile([P, 1], F32)
+        nc.vector.memset(warm[:], 0.0)
+        nc.scalar.activation(out=warm[:], in_=warm[:], func=ACT.Exp)
         nc.vector.memset(logits[:], 0.0)
+        nc.vector.memset(zero[:], 0.0)
         nc.vector.memset(w_planes[:].bitcast(I32), 0)
         nc.vector.memset(ln_raw[:], 0.0)
         nc.vector.memset(minus_half[:], -0.5)
@@ -112,46 +118,9 @@ def tile_dynamicfeaturegroupinglayer_e_kernel(
                 load_x(g)
             load_weight_words(g)
 
-        top = keep.tile([P, 1], F32)
-        nc.vector.reduce_max(out=top[:], in_=logits[:], axis=AXIS.X)
-        minus_alpha_top = keep.tile([P, 1], F32)
-        nc.vector.tensor_scalar_mul(out=minus_alpha_top[:], in0=top[:], scalar1=-ALPHA)
-        powered = keep.tile([P, FEATURES], F32)
-        total = keep.tile([P, 1], F32)
-        nc.scalar.activation(
-            out=powered[:], in_=logits[:], func=ACT.Exp,
-            bias=minus_alpha_top[:], scale=ALPHA, accum_out=total[:],
-        )
-        total_eps = keep.tile([P, 1], F32)
-        nc.vector.tensor_scalar_add(out=total_eps[:], in0=total[:], scalar1=ENTMAX_EPS)
-        log_total = keep.tile([P, 1], F32)
-        nc.scalar.activation(out=log_total[:], in_=total_eps[:], func=ACT.Ln)
-        shift = keep.tile([P, 1], F32)
-        nc.vector.scalar_tensor_tensor(
-            out=shift[:], in0=log_total[:], scalar=-1.0 / ALPHA, in1=top[:],
-            op0=ALU.mult, op1=ALU.subtract,
-        )
-        mask_rows_tp = keep.tile([P, PACK, P], F32)
-        nc.scalar.activation(
-            out=mask_rows_tp[:], in_=logits[:].rearrange("r (p t) -> r t p", t=PACK),
-            func=ACT.Exp, bias=shift[:], scale=1.0,
-        )
-        mask_ps = psum_t.tile([P, PACK, P], F32, tag="t")
-        for t in range(PACK):
-            nc.tensor.transpose(out=mask_ps[:, t, :], in_=mask_rows_tp[:, t, :], identity=identity[:])
         mask_pt = keep.tile([P, mask_rows, PACK], F32)
-        nc.vector.tensor_copy(
-            out=mask_pt[:], in_=mask_ps[:, :, 0:mask_rows].rearrange("p t r -> p r t")
-        )
-
         ln_f32 = keep.tile([P, 4, P], F32)
-        nc.vector.tensor_copy(out=ln_f32[:], in_=ln_raw[:])
-        ln_ps = psum_t.tile([P, 4, P], F32, tag="t")
-        for i in range(4):
-            nc.tensor.transpose(out=ln_ps[:, i, :], in_=ln_f32[:, i, :], identity=identity[:])
         ln_j = keep.tile([P, 4, ln_rows], F32)
-        nc.vector.tensor_copy(out=ln_j[:], in_=ln_ps[:, :, 0:ln_rows])
-
         x_ps = {}
         measured_ps = {}
         stats = {}
@@ -328,6 +297,56 @@ def tile_dynamicfeaturegroupinglayer_e_kernel(
                 out=out[h * P : (h + 1) * P, g * OUTPUTS : (g + 1) * OUTPUTS], in_=out_rows[:]
             )
 
+        def make_masks():
+            top = keep.tile([P, 1], F32)
+            nc.vector.reduce_max(out=top[:], in_=logits[:], axis=AXIS.X)
+            minus_alpha_top = keep.tile([P, 1], F32)
+            nc.vector.tensor_scalar_mul(out=minus_alpha_top[:], in0=top[:], scalar1=-ALPHA)
+            minus_top = keep.tile([P, 1], F32)
+            nc.vector.tensor_scalar_mul(out=minus_top[:], in0=top[:], scalar1=-1.0)
+            minus_inverse_alpha = keep.tile([P, 1], F32)
+            nc.vector.tensor_scalar_add(out=minus_inverse_alpha[:], in0=zero[:], scalar1=-1.0 / ALPHA)
+            powered = keep.tile([P, FEATURES], F32)
+            total = keep.tile([P, 1], F32)
+            nc.scalar.activation(
+                out=powered[:], in_=logits[:], func=ACT.Exp,
+                bias=minus_alpha_top[:], scale=ALPHA, accum_out=total[:],
+            )
+            e_rows_tp = keep.tile([P, PACK, P], F32)
+            nc.scalar.activation(
+                out=e_rows_tp[:], in_=logits[:].rearrange("r (p t) -> r t p", t=PACK),
+                func=ACT.Exp, bias=minus_top[:], scale=1.0,
+            )
+            nc.scalar.activation(out=warm[:], in_=warm[:], func=ACT.Sigmoid)
+            total_eps = keep.tile([P, 1], F32)
+            nc.gpsimd.tensor_scalar(
+                out=total_eps[:], in0=total[:], scalar1=1.0, scalar2=ENTMAX_EPS,
+                op0=ALU.mult, op1=ALU.add,
+            )
+            shrink = keep.tile([P, 1], F32)
+            nc.gpsimd.tensor_tensor(
+                out=shrink[:], in0=total_eps[:], in1=minus_inverse_alpha[:], op=ALU.pow
+            )
+            mask_rows_tp = keep.tile([P, PACK, P], F32)
+            nc.vector.tensor_scalar_mul(out=mask_rows_tp[:], in0=e_rows_tp[:], scalar1=shrink[:])
+            mask_ps = psum_t.tile([P, PACK, P], F32, tag="t")
+            for t in range(PACK):
+                nc.tensor.transpose(
+                    out=mask_ps[:, t, :], in_=mask_rows_tp[:, t, :], identity=identity[:]
+                )
+            nc.vector.tensor_copy(
+                out=mask_pt[:], in_=mask_ps[:, :, 0:mask_rows].rearrange("p t r -> p r t")
+            )
+
+        def widen_layer_norm_vectors():
+            nc.scalar.copy(out=ln_f32[:], in_=ln_raw[:])
+
+        def transpose_layer_norm_vectors():
+            ln_ps = psum_t.tile([P, 4, P], F32, tag="t")
+            for i in range(4):
+                nc.tensor.transpose(out=ln_ps[:, i, :], in_=ln_f32[:, i, :], identity=identity[:])
+            nc.scalar.copy(out=ln_j[:], in_=ln_ps[:, :, 0:ln_rows])
+
         def in_range(index):
             return 0 <= index < PAIRS
 
@@ -341,7 +360,10 @@ def tile_dynamicfeaturegroupinglayer_e_kernel(
             return in_range(k) and k % MASKS == MASKS - 1
 
         with tc.manual_schedule():
-            for k in range(-X_AHEAD, PAIRS + STORE_BEHIND):
+            transpose_x(0)
+            make_masks()
+            widen_layer_norm_vectors()
+            for k in range(-WEIGH_AHEAD, PAIRS + STORE_BEHIND):
                 if in_range(k - ACTIVATE_BEHIND):
                     transpose_normed(k - ACTIVATE_BEHIND)
                 if in_range(k):
@@ -350,8 +372,10 @@ def tile_dynamicfeaturegroupinglayer_e_kernel(
                     products[k - PROJECT_AGAIN_BEHIND] = project(k - PROJECT_AGAIN_BEHIND, psum_normalise)
                 if in_range(k - ADD_MASKS_BEHIND):
                     add_masks(k - ADD_MASKS_BEHIND)
-                if first_of_group(k + X_AHEAD):
+                if first_of_group(k + X_AHEAD) and k + X_AHEAD > 0:
                     transpose_x((k + X_AHEAD) // PAIRS_PER_GROUP)
+                if k == LN_VECTORS_STEP:
+                    transpose_layer_norm_vectors()
 
                 if in_range(k + WEIGH_AHEAD):
                     weigh(k + WEIGH_AHEAD)

@@ -227,6 +227,9 @@ def tile_dynamicfeaturegroupinglayer_e_kernel(
             rstd[u] = scale
             minus_mean_rstd[u] = bias
 
+        def on_vector(k, w):
+            return w == 1 and k % MASKS == MASKS - 1
+
         def normalise(k):
             u, m = k // MASKS, k % MASKS
             if m == 0:
@@ -234,11 +237,18 @@ def tile_dynamicfeaturegroupinglayer_e_kernel(
                 normed[u] = unit_normed
             for w in range(2):
                 column = 2 * m + w
-                nc.scalar.activation(
-                    out=normed[u][:, w, m, :], in_=products[k][w][:], func=ACT.Identity,
-                    scale=rstd[u][:, column : column + 1],
-                    bias=minus_mean_rstd[u][:, column : column + 1],
-                )
+                if on_vector(k, w):
+                    nc.vector.tensor_scalar(
+                        out=normed[u][:, w, m, :], in0=products[k][w][:],
+                        scalar1=mean_var[u][:, m, w, 0:1], scalar2=rstd[u][:, column : column + 1],
+                        op0=ALU.subtract, op1=ALU.mult,
+                    )
+                else:
+                    nc.scalar.activation(
+                        out=normed[u][:, w, m, :], in_=products[k][w][:], func=ACT.Identity,
+                        scale=rstd[u][:, column : column + 1],
+                        bias=minus_mean_rstd[u][:, column : column + 1],
+                    )
 
         def transpose_normed(q):
             u, c = q // CHUNKS, q % CHUNKS
@@ -377,6 +387,8 @@ def tile_dynamicfeaturegroupinglayer_e_kernel(
                 if k == LN_VECTORS_STEP:
                     transpose_layer_norm_vectors()
 
+                if in_range(k - NORMALISE_BEHIND):
+                    normalise(k - NORMALISE_BEHIND)
                 if in_range(k + WEIGH_AHEAD):
                     weigh(k + WEIGH_AHEAD)
                 if last_of_unit(k - STORE_BEHIND):
@@ -391,7 +403,5 @@ def tile_dynamicfeaturegroupinglayer_e_kernel(
                 if in_range(k - MULTIPLY_BEHIND):
                     multiply(k - MULTIPLY_BEHIND)
 
-                if in_range(k - NORMALISE_BEHIND):
-                    normalise(k - NORMALISE_BEHIND)
                 if in_range(k - ACTIVATE_BEHIND):
                     activate(k - ACTIVATE_BEHIND)

@@ -228,7 +228,7 @@ def tile_dynamicfeaturegroupinglayer_e_kernel(
             minus_mean_rstd[u] = bias
 
         def on_vector(k, w):
-            return w == 1 and k % MASKS == MASKS - 1
+            return w == 1 and (k % MASKS == MASKS - 1 or k + NORMALISE_BEHIND >= PAIRS)
 
         def normalise(k):
             u, m = k // MASKS, k % MASKS
@@ -280,23 +280,34 @@ def tile_dynamicfeaturegroupinglayer_e_kernel(
 
         def multiply(q):
             u, c = q // CHUNKS, q % CHUNKS
-            nc.gpsimd.tensor_tensor(
+            if u < UNITS - 1:
+                nc.gpsimd.tensor_tensor(
+                    out=value[u][:, c, :], in0=value[u][:, c, :], in1=gate[u][:, c, :], op=ALU.mult
+                )
+                return
+            nc.vector.tensor_tensor(
                 out=value[u][:, c, :], in0=value[u][:, c, :], in1=gate[u][:, c, :], op=ALU.mult
             )
+            for width in (2 * P, P):
+                nc.vector.tensor_tensor(
+                    out=value[u][:, c, 0:width], in0=value[u][:, c, 0:width],
+                    in1=value[u][:, c, width : 2 * width], op=ALU.add,
+                )
 
         def add_masks(q):
             u, c = q // CHUNKS, q % CHUNKS
             if c == 0:
                 sums_ps = psum_sum.tile([P, OUTPUTS], F32)
                 out_ps[u] = sums_ps
-            for m in range(MASKS):
+            left = MASKS if u < UNITS - 1 else 1
+            for m in range(left):
                 nc.tensor.matmul(
                     out=out_ps[u][:, c * P : (c + 1) * P],
                     lhsT=value[u][:, c, m * P : (m + 1) * P],
                     rhs=identity[:],
                     is_transpose=True,
                     start=(m == 0),
-                    stop=(m == MASKS - 1),
+                    stop=(m == left - 1),
                 )
 
         def store(u):

@@ -228,7 +228,7 @@ def tile_dynamicfeaturegroupinglayer_e_kernel(
             minus_mean_rstd[u] = bias
 
         def on_vector(k, w):
-            return w == 1 and (k % MASKS == MASKS - 1 or k + NORMALISE_BEHIND >= PAIRS)
+            return w == 1 and (k % PAIRS_PER_GROUP == PAIRS_PER_GROUP - 1 or k + NORMALISE_BEHIND >= PAIRS)
 
         def normalise(k):
             u, m = k // MASKS, k % MASKS

@@ -33,7 +33,7 @@ PAIRS_PER_GROUP = HALVES * MASKS
 LN_VECTORS_STEP = 1
 X_AHEAD = 6
 WEIGH_AHEAD = 5
-QUANTISE_AHEAD = 2
+QUANTISE_AHEAD = 1
 PROJECT_AGAIN_BEHIND = 5
 NORMALISE_BEHIND = 6
 ACTIVATE_BEHIND = 10
@@ -406,11 +406,12 @@ def tile_dynamicfeaturegroupinglayer_e_kernel(
                     store((k - STORE_BEHIND) // MASKS)
                 if in_range(k):
                     measure(k)
+                if first_of_unit(k + QUANTISE_AHEAD):
+                    quantise((k + QUANTISE_AHEAD) // MASKS)
+                if in_range(k):
                     aggregate(k)
                 if last_of_unit(k):
                     scale_and_bias(k // MASKS)
-                if first_of_unit(k + QUANTISE_AHEAD):
-                    quantise((k + QUANTISE_AHEAD) // MASKS)
                 if in_range(k - MULTIPLY_BEHIND):
                     multiply(k - MULTIPLY_BEHIND)
 

@@ -1,3 +1,4 @@
+import math
 from contextlib import ExitStack
 
 import concourse.mybir as mybir
@@ -128,7 +129,10 @@ def tile_dynamicfeaturegroupinglayer_e_kernel(
         weighted = {}
         a_words = {}
         a_planes = {}
-        mean_var = {}
+        unit_sums = {}
+        differences = {}
+        minus_means = {}
+        totals = {}
         rstd = {}
         minus_mean_rstd = {}
         normed = {}
@@ -194,41 +198,54 @@ def tile_dynamicfeaturegroupinglayer_e_kernel(
             return pair
 
         def measure(k):
-            six = small.tile([P, 2, 6], F32)
-            for w in range(2):
-                nc.vector.bn_stats(out=six[:, w, :], in_=measured_ps[k][w][:])
-            stats[k] = six
-
-        def aggregate(k):
             u, m = k // MASKS, k % MASKS
             if m == 0:
-                unit_mean_var = small.tile([P, MASKS, 2, 2], F32)
-                mean_var[u] = unit_mean_var
+                unit_stats = small.tile([P, 2 * MASKS, 2, 3], F32)
+                stats[u] = unit_stats
             for w in range(2):
-                nc.vector.bn_aggr(out=mean_var[u][:, m, w, :], in_=stats[k][:, w, :])
+                nc.vector.bn_stats(
+                    out=stats[u][:, 2 * m + w].rearrange("p s f -> p (s f)"), in_=measured_ps[k][w][:]
+                )
+
+        def add_up(u):
+            sums = small.tile([P, 2 * MASKS, 2], F32)
+            nc.vector.tensor_reduce(
+                out=sums[:], in_=stats[u][:].rearrange("p i s f -> p i f s")[:, :, 1:3, :],
+                op=ALU.add, axis=AXIS.X,
+            )
+            difference = small.tile([P, 2 * MASKS], F32)
+            nc.vector.tensor_tensor(
+                out=difference[:], in0=stats[u][:, :, 0, 1], in1=stats[u][:, :, 1, 1], op=ALU.subtract
+            )
+            unit_sums[u] = sums
+            differences[u] = difference
+
+        def deviations(u):
+            between = small.tile([P, 2 * MASKS], F32)
+            nc.vector.scalar_tensor_tensor(
+                out=between[:], in0=differences[u][:], scalar=OUTPUTS / 4.0, in1=differences[u][:],
+                op0=ALU.mult, op1=ALU.mult,
+            )
+            minus_mean = small.tile([P, 2 * MASKS], F32)
+            nc.vector.tensor_scalar_mul(out=minus_mean[:], in0=unit_sums[u][:, :, 0], scalar1=-0.5)
+            minus_means[u] = minus_mean
+            total = small.tile([P, 2 * MASKS], F32)
+            nc.vector.scalar_tensor_tensor(
+                out=total[:], in0=unit_sums[u][:, :, 1], scalar=OUTPUTS * LN_EPS, in1=between[:],
+                op0=ALU.add, op1=ALU.add,
+            )
+            totals[u] = total
 
         def scale_and_bias(u):
-            means = mean_var[u][:].rearrange("p m w s -> p (m w) s")[:, :, 0]
-            variances = mean_var[u][:].rearrange("p m w s -> p (m w) s")[:, :, 1]
-            var_eps = small.tile([P, 2 * MASKS], F32)
-            nc.gpsimd.tensor_scalar(
-                out=var_eps[:], in0=variances, scalar1=1.0, scalar2=LN_EPS,
-                op0=ALU.mult, op1=ALU.add,
-            )
             scale = small.tile([P, 2 * MASKS], F32)
-            nc.gpsimd.tensor_tensor(out=scale[:], in0=var_eps[:], in1=minus_half[:], op=ALU.pow)
-            minus_mean = small.tile([P, 2 * MASKS], F32)
-            nc.gpsimd.tensor_scalar(
-                out=minus_mean[:], in0=means, scalar1=-1.0, scalar2=0.0,
-                op0=ALU.mult, op1=ALU.add,
-            )
+            nc.gpsimd.tensor_tensor(out=scale[:], in0=totals[u][:], in1=minus_half[:], op=ALU.pow)
             bias = small.tile([P, 2 * MASKS], F32)
-            nc.gpsimd.tensor_tensor(out=bias[:], in0=minus_mean[:], in1=scale[:], op=ALU.mult)
+            nc.gpsimd.tensor_tensor(out=bias[:], in0=minus_means[u][:], in1=scale[:], op=ALU.mult)
             rstd[u] = scale
             minus_mean_rstd[u] = bias
 
         def on_vector(k, w):
-            return w == 1 and (k % PAIRS_PER_GROUP == PAIRS_PER_GROUP - 1 or k + NORMALISE_BEHIND >= PAIRS)
+            return w == 1 and (k % MASKS == MASKS - 1 or k + NORMALISE_BEHIND >= PAIRS)
 
         def normalise(k):
             u, m = k // MASKS, k % MASKS
@@ -240,8 +257,9 @@ def tile_dynamicfeaturegroupinglayer_e_kernel(
                 if on_vector(k, w):
                     nc.vector.tensor_scalar(
                         out=normed[u][:, w, m, :], in0=products[k][w][:],
-                        scalar1=mean_var[u][:, m, w, 0:1], scalar2=rstd[u][:, column : column + 1],
-                        op0=ALU.subtract, op1=ALU.mult,
+                        scalar1=rstd[u][:, column : column + 1],
+                        scalar2=minus_mean_rstd[u][:, column : column + 1],
+                        op0=ALU.mult, op1=ALU.add,
                     )
                 else:
                     nc.scalar.activation(
@@ -366,7 +384,11 @@ def tile_dynamicfeaturegroupinglayer_e_kernel(
             ln_ps = psum_t.tile([P, 4, P], F32, tag="t")
             for i in range(4):
                 nc.tensor.transpose(out=ln_ps[:, i, :], in_=ln_f32[:, i, :], identity=identity[:])
-            nc.scalar.copy(out=ln_j[:], in_=ln_ps[:, :, 0:ln_rows])
+            for i in range(4):
+                nc.scalar.activation(
+                    out=ln_j[:, i, :], in_=ln_ps[:, i, 0:ln_rows], func=ACT.Identity,
+                    scale=math.sqrt(OUTPUTS) if i % 2 == 0 else 1.0,
+                )
 
         def in_range(index):
             return 0 <= index < PAIRS
@@ -400,17 +422,17 @@ def tile_dynamicfeaturegroupinglayer_e_kernel(
 
                 if in_range(k - NORMALISE_BEHIND):
                     normalise(k - NORMALISE_BEHIND)
-                if in_range(k + WEIGH_AHEAD):
-                    weigh(k + WEIGH_AHEAD)
                 if last_of_unit(k - STORE_BEHIND):
                     store((k - STORE_BEHIND) // MASKS)
+                if in_range(k + WEIGH_AHEAD):
+                    weigh(k + WEIGH_AHEAD)
                 if in_range(k):
                     measure(k)
                 if first_of_unit(k + QUANTISE_AHEAD):
                     quantise((k + QUANTISE_AHEAD) // MASKS)
-                if in_range(k):
-                    aggregate(k)
                 if last_of_unit(k):
+                    add_up(k // MASKS)
+                    deviations(k // MASKS)
                     scale_and_bias(k // MASKS)
                 if in_range(k - MULTIPLY_BEHIND):
                     multiply(k - MULTIPLY_BEHIND)

@@ -28,19 +28,20 @@ ENTMAX_EPS = 1e-5
 LN_EPS = 1e-5
 X_LOAD_GROUPS = 2
 UNITS = GROUPS * HALVES
+PRODUCTS = 2 * MASKS
 PAIRS = UNITS * MASKS
 PAIRS_PER_GROUP = HALVES * MASKS
 
-LN_VECTORS_STEP = 1
-X_AHEAD = 6
-WEIGH_AHEAD = 5
-QUANTISE_AHEAD = 1
-PROJECT_AGAIN_BEHIND = 5
-NORMALISE_BEHIND = 6
-ACTIVATE_BEHIND = 10
-MULTIPLY_BEHIND = 11
-ADD_MASKS_BEHIND = 14
-STORE_BEHIND = 15
+SLOTS = PRODUCTS + 2 * CHUNKS
+PAIR_SLOTS = SLOTS // MASKS
+MEASURED_EARLY = 20
+PAIR_SHIFT = (0, -1, -1, -2)
+WEIGHED_EARLY = MASKS
+ADDED_LATE = 10
+STORED_LATE = 3
+VECTOR_PASS = 0
+
+LN_VECTORS_SLOT = -16
 
 FLOPS = 2 * 2 * BATCH * GROUPS * MASKS * FEATURES * OUTPUTS
 
@@ -64,8 +65,7 @@ def tile_dynamicfeaturegroupinglayer_e_kernel(
         out_pool = ctx.enter_context(tc.tile_pool(name="out_pool", bufs=2))
         psum_x = ctx.enter_context(tc.psum_pool(name="psum_x", bufs=1))
         psum_measure = ctx.enter_context(tc.psum_pool(name="psum_measure", bufs=2))
-        psum_normalise = ctx.enter_context(tc.psum_pool(name="psum_normalise", bufs=2))
-        psum_t = ctx.enter_context(tc.psum_pool(name="psum_t", bufs=2))
+        psum_scalar = ctx.enter_context(tc.psum_pool(name="psum_scalar", bufs=4))
         psum_sum = ctx.enter_context(tc.psum_pool(name="psum_sum", bufs=1))
 
         logits = keep.tile([P, FEATURES], BF16)
@@ -139,7 +139,7 @@ def tile_dynamicfeaturegroupinglayer_e_kernel(
         gate = {}
         value = {}
         out_ps = {}
-        normed_ps = {}
+        fed_ps = {}
 
         def transpose_x(g):
             words_ps = psum_x.tile([P, HALVES, 2, P], F32)
@@ -179,33 +179,29 @@ def tile_dynamicfeaturegroupinglayer_e_kernel(
             a_words[u] = words
             a_planes[u] = planes
 
-        def project(k, pool):
-            g, u, m = k // PAIRS_PER_GROUP, k // MASKS, k % MASKS
+        def project(i, pool):
+            u, m, w = i // PRODUCTS, i // 2 % MASKS, i % 2
             rows = slice(m * P, (m + 1) * P)
-            pair = []
-            for w in range(2):
-                h_ps = pool.tile([P, OUTPUTS], F32, tag="h")
-                nc.tensor.matmul_mx(
-                    out=h_ps[:],
-                    lhsT=a_words[u][:, rows].bitcast(FP8X4),
-                    lhsT_scale=a_planes[u][:, rows],
-                    rhs=w_words[:, w, g, :].bitcast(FP8X4),
-                    rhs_scale=w_planes[:, w, g, :],
-                    start=True,
-                    stop=True,
-                )
-                pair.append(h_ps)
-            return pair
+            h_ps = pool.tile([P, OUTPUTS], F32, tag="h")
+            nc.tensor.matmul_mx(
+                out=h_ps[:],
+                lhsT=a_words[u][:, rows].bitcast(FP8X4),
+                lhsT_scale=a_planes[u][:, rows],
+                rhs=w_words[:, w, u // HALVES, :].bitcast(FP8X4),
+                rhs_scale=w_planes[:, w, u // HALVES, :],
+                start=True,
+                stop=True,
+            )
+            return h_ps
 
-        def measure(k):
-            u, m = k // MASKS, k % MASKS
-            if m == 0:
+        def measure(i, h_ps):
+            u = i // PRODUCTS
+            if i % PRODUCTS == 0:
                 unit_stats = small.tile([P, 2 * MASKS, 2, 3], F32)
                 stats[u] = unit_stats
-            for w in range(2):
-                nc.vector.bn_stats(
-                    out=stats[u][:, 2 * m + w].rearrange("p s f -> p (s f)"), in_=measured_ps[k][w][:]
-                )
+            nc.vector.bn_stats(
+                out=stats[u][:, i % PRODUCTS].rearrange("p s f -> p (s f)"), in_=h_ps[:]
+            )
 
         def add_up(u):
             sums = small.tile([P, 2 * MASKS, 2], F32)
@@ -244,88 +240,86 @@ def tile_dynamicfeaturegroupinglayer_e_kernel(
             rstd[u] = scale
             minus_mean_rstd[u] = bias
 
-        def on_vector(k, w):
-            return w == 1 and (k % MASKS == MASKS - 1 or k + NORMALISE_BEHIND >= PAIRS)
-
-        def normalise(k):
-            u, m = k // MASKS, k % MASKS
-            if m == 0:
+        def normalise(i, h_ps, on_vector):
+            u, m, w = i // PRODUCTS, i // 2 % MASKS, i % 2
+            column = i % PRODUCTS
+            if u not in normed:
                 unit_normed = norm_pool.tile([P, 2, MASKS, OUTPUTS], F32)
                 normed[u] = unit_normed
-            for w in range(2):
-                column = 2 * m + w
-                if on_vector(k, w):
-                    nc.vector.tensor_scalar(
-                        out=normed[u][:, w, m, :], in0=products[k][w][:],
-                        scalar1=rstd[u][:, column : column + 1],
-                        scalar2=minus_mean_rstd[u][:, column : column + 1],
-                        op0=ALU.mult, op1=ALU.add,
-                    )
-                else:
-                    nc.scalar.activation(
-                        out=normed[u][:, w, m, :], in_=products[k][w][:], func=ACT.Identity,
-                        scale=rstd[u][:, column : column + 1],
-                        bias=minus_mean_rstd[u][:, column : column + 1],
-                    )
+            scale = rstd[u][:, column : column + 1]
+            bias = minus_mean_rstd[u][:, column : column + 1]
+            if on_vector:
+                nc.vector.tensor_scalar(
+                    out=normed[u][:, w, m, :], in0=h_ps[:], scalar1=scale, scalar2=bias,
+                    op0=ALU.mult, op1=ALU.add,
+                )
+            else:
+                nc.scalar.activation(
+                    out=normed[u][:, w, m, :], in_=h_ps[:], func=ACT.Identity, scale=scale, bias=bias
+                )
 
-        def transpose_normed(q):
+        def transpose_normed(q, w):
             u, c = q // CHUNKS, q % CHUNKS
-            normed_ps[q] = []
-            for w in range(2):
-                chunk_ps = psum_t.tile([P, MASKS, P], F32, tag="t")
-                for m in range(MASKS):
-                    nc.tensor.transpose(
-                        out=chunk_ps[:, m, :],
-                        in_=normed[u][:, w, m, c * P : (c + 1) * P],
-                        identity=identity[:],
-                    )
-                normed_ps[q].append(chunk_ps)
+            chunk_ps = psum_scalar.tile([P, MASKS, P], F32, tag="h")
+            for m in range(MASKS):
+                nc.tensor.transpose(
+                    out=chunk_ps[:, m, :],
+                    in_=normed[u][:, w, m, c * P : (c + 1) * P],
+                    identity=identity[:],
+                )
+            return chunk_ps
 
-        def activate(q):
+        def activate(q, w, chunk_ps, on_vector):
             u, c = q // CHUNKS, q % CHUNKS
-            if c == 0:
+            if u not in gate:
                 unit_gate = act_pool.tile([P, CHUNKS, MASKS * P], F32)
                 unit_value = act_pool.tile([P, CHUNKS, MASKS * P], F32)
                 gate[u] = unit_gate
                 value[u] = unit_value
             row = CHUNKS * (u // HALVES) + c
-            for w, (func, result) in enumerate(((ACT.Sigmoid, gate[u]), (ACT.Relu, value[u]))):
-                nc.scalar.activation(
-                    out=result[:, c, :], in_=normed_ps[q][w][:].rearrange("j m b -> j (m b)"),
-                    func=func,
-                    scale=ln_j[:, 2 * w, row : row + 1], bias=ln_j[:, 2 * w + 1, row : row + 1],
+            chunk = chunk_ps[:].rearrange("j m b -> j (m b)")
+            if on_vector:
+                nc.vector.tensor_scalar(
+                    out=value[u][:, c, :], in0=chunk,
+                    scalar1=ln_j[:, 2, row : row + 1], scalar2=ln_j[:, 3, row : row + 1],
+                    op0=ALU.mult, op1=ALU.add,
                 )
+                return
+            nc.scalar.activation(
+                out=(gate, value)[w][u][:, c, :], in_=chunk,
+                func=(ACT.Sigmoid, ACT.Relu)[w],
+                scale=ln_j[:, 2 * w, row : row + 1], bias=ln_j[:, 2 * w + 1, row : row + 1],
+            )
 
         def multiply(q):
             u, c = q // CHUNKS, q % CHUNKS
-            if u < UNITS - 1:
+            if u == UNITS - 1:
+                nc.vector.scalar_tensor_tensor(
+                    out=value[u][:, c, :], in0=value[u][:, c, :], scalar=0.0, in1=gate[u][:, c, :],
+                    op0=ALU.max, op1=ALU.mult,
+                )
+            else:
                 nc.gpsimd.tensor_tensor(
                     out=value[u][:, c, :], in0=value[u][:, c, :], in1=gate[u][:, c, :], op=ALU.mult
-                )
-                return
-            nc.vector.tensor_tensor(
-                out=value[u][:, c, :], in0=value[u][:, c, :], in1=gate[u][:, c, :], op=ALU.mult
-            )
-            for width in (2 * P, P):
-                nc.vector.tensor_tensor(
-                    out=value[u][:, c, 0:width], in0=value[u][:, c, 0:width],
-                    in1=value[u][:, c, width : 2 * width], op=ALU.add,
                 )
 
         def add_masks(q):
             u, c = q // CHUNKS, q % CHUNKS
             if c == 0:
-                sums_ps = psum_sum.tile([P, OUTPUTS], F32)
-                out_ps[u] = sums_ps
-            left = MASKS if u < UNITS - 1 else 1
-            for m in range(left):
+                if u < UNITS - 1:
+                    sums_ps = psum_sum.tile([P, OUTPUTS], F32)
+                    out_ps[u] = sums_ps
+                else:
+                    last_sums_ps = psum_measure.tile([P, OUTPUTS], F32, tag="h")
+                    out_ps[u] = last_sums_ps
+            for m in range(MASKS):
                 nc.tensor.matmul(
                     out=out_ps[u][:, c * P : (c + 1) * P],
                     lhsT=value[u][:, c, m * P : (m + 1) * P],
                     rhs=identity[:],
                     is_transpose=True,
                     start=(m == 0),
-                    stop=(m == left - 1),
+                    stop=(m == MASKS - 1),
                 )
 
         def store(u):
@@ -368,7 +362,7 @@ def tile_dynamicfeaturegroupinglayer_e_kernel(
             )
             mask_rows_tp = keep.tile([P, PACK, P], F32)
             nc.vector.tensor_scalar_mul(out=mask_rows_tp[:], in0=e_rows_tp[:], scalar1=shrink[:])
-            mask_ps = psum_t.tile([P, PACK, P], F32, tag="t")
+            mask_ps = psum_scalar.tile([P, PACK, P], F32, tag="h")
             for t in range(PACK):
                 nc.tensor.transpose(
                     out=mask_ps[:, t, :], in_=mask_rows_tp[:, t, :], identity=identity[:]
@@ -381,7 +375,7 @@ def tile_dynamicfeaturegroupinglayer_e_kernel(
             nc.scalar.copy(out=ln_f32[:], in_=ln_raw[:])
 
         def transpose_layer_norm_vectors():
-            ln_ps = psum_t.tile([P, 4, P], F32, tag="t")
+            ln_ps = psum_scalar.tile([P, 4, P], F32, tag="h")
             for i in range(4):
                 nc.tensor.transpose(out=ln_ps[:, i, :], in_=ln_f32[:, i, :], identity=identity[:])
             for i in range(4):
@@ -390,52 +384,72 @@ def tile_dynamicfeaturegroupinglayer_e_kernel(
                     scale=math.sqrt(OUTPUTS) if i % 2 == 0 else 1.0,
                 )
 
-        def in_range(index):
-            return 0 <= index < PAIRS
+        def on_scalar(s):
+            u, j = s // SLOTS, s % SLOTS
+            if j >= PRODUCTS:
+                return u, None, CHUNKS * u + (j - PRODUCTS) // 2, j % 2
+            if u == UNITS - 1:
+                return u, PRODUCTS * u + j, None, j % 2
+            return u, PRODUCTS * u + 2 * (j % MASKS) + j // MASKS, None, j // MASKS
 
-        def first_of_group(k):
-            return in_range(k) and k % PAIRS_PER_GROUP == 0
+        def feed(s):
+            u, i, q, w = on_scalar(s)
+            fed_ps[s] = project(i, psum_scalar) if q is None else transpose_normed(q, w)
 
-        def first_of_unit(k):
-            return in_range(k) and k % MASKS == 0
+        def take(s):
+            u, i, q, w = on_scalar(s)
+            if q is None:
+                normalise(i, fed_ps[s], w == 1 if u == UNITS - 1 else s % SLOTS == VECTOR_PASS)
+            else:
+                activate(q, w, fed_ps[s], u == UNITS - 1 and w == 1 and q % 2 == 0)
 
-        def last_of_unit(k):
-            return in_range(k) and k % MASKS == MASKS - 1
-
+        pair_at = {
+            PAIR_SLOTS * k - MEASURED_EARLY + PAIR_SHIFT[k % MASKS]: k
+            for k in range(-WEIGHED_EARLY, PAIRS)
+        }
         with tc.manual_schedule():
             transpose_x(0)
             make_masks()
             widen_layer_norm_vectors()
-            for k in range(-WEIGH_AHEAD, PAIRS + STORE_BEHIND):
-                if in_range(k - ACTIVATE_BEHIND):
-                    transpose_normed(k - ACTIVATE_BEHIND)
-                if in_range(k):
-                    measured_ps[k] = project(k, psum_measure)
-                if in_range(k - PROJECT_AGAIN_BEHIND):
-                    products[k - PROJECT_AGAIN_BEHIND] = project(k - PROJECT_AGAIN_BEHIND, psum_normalise)
-                if in_range(k - ADD_MASKS_BEHIND):
-                    add_masks(k - ADD_MASKS_BEHIND)
-                if first_of_group(k + X_AHEAD) and k + X_AHEAD > 0:
-                    transpose_x((k + X_AHEAD) // PAIRS_PER_GROUP)
-                if k == LN_VECTORS_STEP:
+            for s in range(min(pair_at), SLOTS * UNITS + ADDED_LATE + 2):
+                k = pair_at.get(s)
+                before = pair_at.get(s - 1)
+                added = s - ADDED_LATE - PRODUCTS
+
+                if s == LN_VECTORS_SLOT:
                     transpose_layer_norm_vectors()
+                if k is not None and k >= 0:
+                    for i in (2 * k, 2 * k + 1):
+                        measured_ps[i] = project(i, psum_measure)
+                if 0 <= s < SLOTS * UNITS:
+                    feed(s)
+                if added > 0 and added % 2 == 1 and added % SLOTS < 2 * CHUNKS and added // SLOTS < UNITS:
+                    add_masks(CHUNKS * (added // SLOTS) + added % SLOTS // 2)
 
-                if in_range(k - NORMALISE_BEHIND):
-                    normalise(k - NORMALISE_BEHIND)
-                if last_of_unit(k - STORE_BEHIND):
-                    store((k - STORE_BEHIND) // MASKS)
-                if in_range(k + WEIGH_AHEAD):
-                    weigh(k + WEIGH_AHEAD)
-                if in_range(k):
-                    measure(k)
-                if first_of_unit(k + QUANTISE_AHEAD):
-                    quantise((k + QUANTISE_AHEAD) // MASKS)
-                if last_of_unit(k):
-                    add_up(k // MASKS)
-                    deviations(k // MASKS)
-                    scale_and_bias(k // MASKS)
-                if in_range(k - MULTIPLY_BEHIND):
-                    multiply(k - MULTIPLY_BEHIND)
-
-                if in_range(k - ACTIVATE_BEHIND):
-                    activate(k - ACTIVATE_BEHIND)
+                if k is not None:
+                    if k + WEIGHED_EARLY < PAIRS:
+                        weigh(k + WEIGHED_EARLY)
+                    if k % MASKS == 0 and k // MASKS >= STORED_LATE:
+                        store(k // MASKS - STORED_LATE)
+                    if k >= 0:
+                        measure(2 * k, measured_ps[2 * k])
+                if before is not None:
+                    weighed = before + WEIGHED_EARLY
+                    if weighed % PAIRS_PER_GROUP == PAIRS_PER_GROUP - 1 and weighed + 1 < PAIRS:
+                        transpose_x((weighed + 1) // PAIRS_PER_GROUP)
+                    if before >= 0:
+                        measure(2 * before + 1, measured_ps[2 * before + 1])
+                    if before % MASKS == MASKS - 1:
+                        u = before // MASKS
+                        if u + 1 < UNITS:
+                            quantise(u + 1)
+                        if u >= 0:
+                            add_up(u)
+                            deviations(u)
+                            scale_and_bias(u)
+                if s > max(pair_at) and added % SLOTS == 2 * CHUNKS and added // SLOTS >= UNITS - STORED_LATE:
+                    store(added // SLOTS)
+                if 0 <= s < SLOTS * UNITS:
+                    take(s)
+                    if s % SLOTS >= PRODUCTS and s % 2 == 1:
+                        multiply(CHUNKS * (s // SLOTS) + (s % SLOTS - PRODUCTS) // 2)

@@ -34,14 +34,16 @@ PAIRS_PER_GROUP = HALVES * MASKS
 
 SLOTS = PRODUCTS + 2 * CHUNKS
 PAIR_SLOTS = SLOTS // MASKS
-MEASURED_EARLY = 20
-PAIR_SHIFT = (0, -1, -1, -2)
+MEASURED_EARLY = 22
+PAIR_SHIFT = (0, -1, -2, -1)
 WEIGHED_EARLY = MASKS
-ADDED_LATE = 10
+ADDED_LATE = 22
 STORED_LATE = 3
-VECTOR_PASS = 0
-
+STORE_PAIR = 2
+VECTOR_PASS = 2
 LN_VECTORS_SLOT = -16
+LAST_PASS = SLOTS * (UNITS - 1)
+EARLY_PASSES = 2
 
 FLOPS = 2 * 2 * BATCH * GROUPS * MASKS * FEATURES * OUTPUTS
 
@@ -305,16 +307,17 @@ def tile_dynamicfeaturegroupinglayer_e_kernel(
 
         def add_masks(q):
             u, c = q // CHUNKS, q % CHUNKS
-            if c == 0:
+            width = chunks_together(u)
+            if c % width == 0:
                 if u < UNITS - 1:
                     sums_ps = psum_sum.tile([P, OUTPUTS], F32)
-                    out_ps[u] = sums_ps
+                    out_ps[q] = sums_ps
                 else:
                     last_sums_ps = psum_measure.tile([P, OUTPUTS], F32, tag="h")
-                    out_ps[u] = last_sums_ps
+                    out_ps[q] = last_sums_ps
             for m in range(MASKS):
                 nc.tensor.matmul(
-                    out=out_ps[u][:, c * P : (c + 1) * P],
+                    out=out_ps[q - c % width][:, c % width * P : (c % width + 1) * P],
                     lhsT=value[u][:, c, m * P : (m + 1) * P],
                     rhs=identity[:],
                     is_transpose=True,
@@ -322,12 +325,21 @@ def tile_dynamicfeaturegroupinglayer_e_kernel(
                     stop=(m == MASKS - 1),
                 )
 
-        def store(u):
+        def chunks_together(u):
+            return CHUNKS // 2 if u == UNITS - 1 else CHUNKS
+
+        def store(q):
+            u, c = q // CHUNKS, q % CHUNKS
+            width = chunks_together(u) * P
             g, h = u // HALVES, u % HALVES
             out_rows = out_pool.tile([P, OUTPUTS], F32)
-            nc.vector.tensor_copy(out=out_rows[:], in_=out_ps[u][:])
+            if u < UNITS - 1:
+                nc.vector.tensor_copy(out=out_rows[:, 0:width], in_=out_ps[q][:, 0:width])
+            else:
+                nc.scalar.copy(out=out_rows[:, 0:width], in_=out_ps[q][:, 0:width])
+            column = g * OUTPUTS + c * P
             nc.sync.dma_start(
-                out=out[h * P : (h + 1) * P, g * OUTPUTS : (g + 1) * OUTPUTS], in_=out_rows[:]
+                out=out[h * P : (h + 1) * P, column : column + width], in_=out_rows[:, 0:width]
             )
 
         def make_masks():
@@ -384,24 +396,35 @@ def tile_dynamicfeaturegroupinglayer_e_kernel(
                     scale=math.sqrt(OUTPUTS) if i % 2 == 0 else 1.0,
                 )
 
-        def on_scalar(s):
+        def task(s):
             u, j = s // SLOTS, s % SLOTS
-            if j >= PRODUCTS:
-                return u, None, CHUNKS * u + (j - PRODUCTS) // 2, j % 2
-            if u == UNITS - 1:
-                return u, PRODUCTS * u + j, None, j % 2
-            return u, PRODUCTS * u + 2 * (j % MASKS) + j // MASKS, None, j // MASKS
+            if j < PRODUCTS:
+                return u, PRODUCTS * u + 2 * (j % MASKS) + j // MASKS, None, j // MASKS
+            return u, None, CHUNKS * u + 2 * ((j - PRODUCTS) // 4) + j % 2, j // 2 % 2
+
+        def passes(s):
+            if LAST_PASS - PRODUCTS <= s < LAST_PASS - PRODUCTS + EARLY_PASSES:
+                return [s, s + PRODUCTS]
+            if LAST_PASS <= s < LAST_PASS + EARLY_PASSES:
+                return []
+            return [s]
 
         def feed(s):
-            u, i, q, w = on_scalar(s)
-            fed_ps[s] = project(i, psum_scalar) if q is None else transpose_normed(q, w)
+            u, i, q, w = task(s)
+            if q is not None:
+                fed_ps[s] = transpose_normed(q, w)
+            else:
+                fed_ps[s] = project(i, psum_measure if u == UNITS - 1 and w == 0 else psum_scalar)
 
         def take(s):
-            u, i, q, w = on_scalar(s)
+            u, i, q, w = task(s)
+            last = u == UNITS - 1
             if q is None:
-                normalise(i, fed_ps[s], w == 1 if u == UNITS - 1 else s % SLOTS == VECTOR_PASS)
+                normalise(i, fed_ps[s], w == 0 or s % 4 >= 2 if last else s % SLOTS == VECTOR_PASS)
             else:
-                activate(q, w, fed_ps[s], u == UNITS - 1 and w == 1 and q % 2 == 0)
+                activate(q, w, fed_ps[s], last and w == 1 and q % 2 == 0)
+                if w == 1:
+                    multiply(q)
 
         pair_at = {
             PAIR_SLOTS * k - MEASURED_EARLY + PAIR_SHIFT[k % MASKS]: k
@@ -411,10 +434,10 @@ def tile_dynamicfeaturegroupinglayer_e_kernel(
             transpose_x(0)
             make_masks()
             widen_layer_norm_vectors()
-            for s in range(min(pair_at), SLOTS * UNITS + ADDED_LATE + 2):
+            for s in range(min(pair_at), LAST_PASS + ADDED_LATE + SLOTS):
                 k = pair_at.get(s)
                 before = pair_at.get(s - 1)
-                added = s - ADDED_LATE - PRODUCTS
+                added = s - ADDED_LATE
 
                 if s == LN_VECTORS_SLOT:
                     transpose_layer_norm_vectors()
@@ -422,15 +445,19 @@ def tile_dynamicfeaturegroupinglayer_e_kernel(
                     for i in (2 * k, 2 * k + 1):
                         measured_ps[i] = project(i, psum_measure)
                 if 0 <= s < SLOTS * UNITS:
-                    feed(s)
+                    for t in passes(s):
+                        feed(t)
                 if added > 0 and added % 2 == 1 and added % SLOTS < 2 * CHUNKS and added // SLOTS < UNITS:
                     add_masks(CHUNKS * (added // SLOTS) + added % SLOTS // 2)
 
                 if k is not None:
                     if k + WEIGHED_EARLY < PAIRS:
                         weigh(k + WEIGHED_EARLY)
-                    if k % MASKS == 0 and k // MASKS >= STORED_LATE:
-                        store(k // MASKS - STORED_LATE)
+                    if k % MASKS == 0 and k > 0:
+                        deviations(k // MASKS - 1)
+                        scale_and_bias(k // MASKS - 1)
+                    if k % MASKS == STORE_PAIR and k // MASKS >= STORED_LATE:
+                        store(CHUNKS * (k // MASKS - STORED_LATE))
                     if k >= 0:
                         measure(2 * k, measured_ps[2 * k])
                 if before is not None:
@@ -445,11 +472,14 @@ def tile_dynamicfeaturegroupinglayer_e_kernel(
                             quantise(u + 1)
                         if u >= 0:
                             add_up(u)
+                        if u == UNITS - 1:
                             deviations(u)
                             scale_and_bias(u)
-                if s > max(pair_at) and added % SLOTS == 2 * CHUNKS and added // SLOTS >= UNITS - STORED_LATE:
-                    store(added // SLOTS)
+                u = added // SLOTS
+                if s > max(pair_at) and UNITS > u >= UNITS - STORED_LATE:
+                    for c in range(0, CHUNKS, chunks_together(u)):
+                        if added % SLOTS == 2 * (c + chunks_together(u)):
+                            store(CHUNKS * u + c)
                 if 0 <= s < SLOTS * UNITS:
-                    take(s)
-                    if s % SLOTS >= PRODUCTS and s % 2 == 1:
-                        multiply(CHUNKS * (s // SLOTS) + (s % SLOTS - PRODUCTS) // 2)
+                    for t in passes(s):
+                        take(t)

@@ -26,6 +26,7 @@ CHUNKS = OUTPUTS // P
 ALPHA = 1.1
 ENTMAX_EPS = 1e-5
 LN_EPS = 1e-5
+LOGIT_BLOCK = 32
 X_LOAD_GROUPS = 2
 UNITS = GROUPS * HALVES
 PRODUCTS = 2 * MASKS
@@ -36,6 +37,7 @@ SLOTS = PRODUCTS + 2 * CHUNKS
 PAIR_SLOTS = SLOTS // MASKS
 MEASURED_EARLY = 22
 PAIR_SHIFT = (0, -1, -2, -1)
+X_LATE = 3
 WEIGHED_EARLY = MASKS
 ADDED_LATE = 22
 STORED_LATE = 3
@@ -82,12 +84,11 @@ def tile_dynamicfeaturegroupinglayer_e_kernel(
         zero = keep.tile([P, 1], F32)
         nc.vector.memset(warm[:], 0.0)
         nc.scalar.activation(out=warm[:], in_=warm[:], func=ACT.Exp)
-        nc.vector.memset(logits[:], 0.0)
         nc.vector.memset(zero[:], 0.0)
         nc.vector.memset(w_planes[:].bitcast(I32), 0)
-        nc.vector.memset(ln_raw[:], 0.0)
-        nc.vector.memset(minus_half[:], -0.5)
         make_identity(nc, identity[:])
+        nc.gpsimd.memset(ln_raw[:], 0.0)
+        nc.gpsimd.memset(minus_half[:], -0.5)
 
         def load_x(first_group):
             cols = slice(first_group * FEATURES, (first_group + X_LOAD_GROUPS) * FEATURES)
@@ -101,7 +102,13 @@ def tile_dynamicfeaturegroupinglayer_e_kernel(
                     in_=weight_words[w][g].rearrange("p n t -> p (n t)").bitcast(I32),
                 )
 
-        nc.sync.dma_start(out=logits[0:mask_rows, :], in_=W_masks.rearrange("g m s -> (g m) s"))
+        logit_rows = W_masks.rearrange("g m s -> (g m) s")
+        for block in range(P // LOGIT_BLOCK):
+            first_row = (mask_rows - LOGIT_BLOCK) * (1 - block % 2)
+            nc.sync.dma_start(
+                out=logits[LOGIT_BLOCK * block : LOGIT_BLOCK * (block + 1), :],
+                in_=logit_rows[first_row : first_row + LOGIT_BLOCK, :],
+            )
         load_x(0)
         for w in range(2):
             for quadrant in range(4):
@@ -155,6 +162,9 @@ def tile_dynamicfeaturegroupinglayer_e_kernel(
                     )
             x_ps[g] = words_ps
 
+        def mask_column(g, m):
+            return (MASKS * g + m + LOGIT_BLOCK) % mask_rows
+
         def weigh(k):
             g, h, m = k // PAIRS_PER_GROUP, k // MASKS % HALVES, k % MASKS
             if m == 0:
@@ -163,7 +173,7 @@ def tile_dynamicfeaturegroupinglayer_e_kernel(
             nc.vector.tensor_tensor(
                 out=weighted[k // MASKS][:, m].rearrange("p b (u e) -> p b u e", e=2),
                 in0=x_ps[g][:].bitcast(BF16)[:, h].rearrange("p u (b e) -> p b u e", e=2),
-                in1=mask_pt[:, MASKS * g + m, :]
+                in1=mask_pt[:, mask_column(g, m), :]
                 .rearrange("p (u e) -> p u e", e=2)
                 .unsqueeze(1)
                 .to_broadcast([P, P, 2, 2]),
@@ -300,9 +310,11 @@ def tile_dynamicfeaturegroupinglayer_e_kernel(
                     out=value[u][:, c, :], in0=value[u][:, c, :], scalar=0.0, in1=gate[u][:, c, :],
                     op0=ALU.max, op1=ALU.mult,
                 )
-            else:
+            elif c % 2 == 1:
+                two = slice(c - 1, c + 1)
                 nc.gpsimd.tensor_tensor(
-                    out=value[u][:, c, :], in0=value[u][:, c, :], in1=gate[u][:, c, :], op=ALU.mult
+                    out=value[u][:, two, :], in0=value[u][:, two, :], in1=gate[u][:, two, :],
+                    op=ALU.mult,
                 )
 
         def add_masks(q):
@@ -437,10 +449,15 @@ def tile_dynamicfeaturegroupinglayer_e_kernel(
             for s in range(min(pair_at), LAST_PASS + ADDED_LATE + SLOTS):
                 k = pair_at.get(s)
                 before = pair_at.get(s - 1)
+                weighed_at = pair_at.get(s - X_LATE)
                 added = s - ADDED_LATE
 
                 if s == LN_VECTORS_SLOT:
                     transpose_layer_norm_vectors()
+                if weighed_at is not None:
+                    weighed = weighed_at + WEIGHED_EARLY
+                    if weighed % PAIRS_PER_GROUP == PAIRS_PER_GROUP - 1 and weighed + 1 < PAIRS:
+                        transpose_x((weighed + 1) // PAIRS_PER_GROUP)
                 if k is not None and k >= 0:
                     for i in (2 * k, 2 * k + 1):
                         measured_ps[i] = project(i, psum_measure)
@@ -461,9 +478,6 @@ def tile_dynamicfeaturegroupinglayer_e_kernel(
                     if k >= 0:
                         measure(2 * k, measured_ps[2 * k])
                 if before is not None:
-                    weighed = before + WEIGHED_EARLY
-                    if weighed % PAIRS_PER_GROUP == PAIRS_PER_GROUP - 1 and weighed + 1 < PAIRS:
-                        transpose_x((weighed + 1) // PAIRS_PER_GROUP)
                     if before >= 0:
                         measure(2 * before + 1, measured_ps[2 * before + 1])
                     if before % MASKS == MASKS - 1:

@@ -77,6 +77,7 @@ def tile_dynamicfeaturegroupinglayer_e_kernel(
         w_planes = keep.tile([P, 2, GROUPS, OUTPUTS], U8, align_bytes=64)
         w_words = keep.tile([P, 2, GROUPS, OUTPUTS], U32, align_bytes=64)
         x_rows = [keep.tile([P, GROUPS * FEATURES], BF16, name="x_rows%d" % h) for h in range(HALVES)]
+        x_split = [keep.tile([P, GROUPS, 2, P], F32, name="x_split%d" % h) for h in range(HALVES)]
         minus_half = keep.tile([P, 2 * MASKS], F32)
         identity = keep.tile([P, P], F32)
 
@@ -123,9 +124,9 @@ def tile_dynamicfeaturegroupinglayer_e_kernel(
             nc.sync.dma_start(
                 out=ln_raw[0:ln_rows, i, :], in_=vector.rearrange("g (c j) -> (g c) j", j=P)
             )
+        for g in range(X_LOAD_GROUPS, GROUPS, X_LOAD_GROUPS):
+            load_x(g)
         for g in range(1, GROUPS):
-            if g % X_LOAD_GROUPS == 0:
-                load_x(g)
             load_weight_words(g)
 
         mask_pt = keep.tile([P, mask_rows, PACK], F32)
@@ -150,14 +151,22 @@ def tile_dynamicfeaturegroupinglayer_e_kernel(
         out_ps = {}
         fed_ps = {}
 
+        def split_x(first, groups):
+            for h in range(HALVES):
+                cols = slice(first * FEATURES, (first + groups) * FEATURES)
+                nc.scalar.copy(
+                    out=x_split[h][:, first : first + groups],
+                    in_=x_rows[h][:, cols].bitcast(F32).rearrange("b (g p u) -> b g u p", p=P, u=2),
+                )
+
         def transpose_x(g):
             words_ps = psum_x.tile([P, HALVES, 2, P], F32)
             for h in range(HALVES):
-                words_of_x = x_rows[h][:].bitcast(F32)
                 for u in range(2):
+                    words = x_rows[h][:].bitcast(F32)[:, u : FEATURES // 2 : 2]
                     nc.tensor.transpose(
                         out=words_ps[:, h, u, :],
-                        in_=words_of_x[:, g * FEATURES // 2 + u : (g + 1) * FEATURES // 2 : 2],
+                        in_=words if g == 0 else x_split[h][:, g, u, :],
                         identity=identity[:],
                     )
             x_ps[g] = words_ps
@@ -445,6 +454,7 @@ def tile_dynamicfeaturegroupinglayer_e_kernel(
         with tc.manual_schedule():
             transpose_x(0)
             make_masks()
+            split_x(1, X_LOAD_GROUPS - 1)
             widen_layer_norm_vectors()
             for s in range(min(pair_at), LAST_PASS + ADDED_LATE + SLOTS):
                 k = pair_at.get(s)
@@ -454,6 +464,8 @@ def tile_dynamicfeaturegroupinglayer_e_kernel(
 
                 if s == LN_VECTORS_SLOT:
                     transpose_layer_norm_vectors()
+                    for g in range(X_LOAD_GROUPS, GROUPS, X_LOAD_GROUPS):
+                        split_x(g, X_LOAD_GROUPS)
                 if weighed_at is not None:
                     weighed = weighed_at + WEIGHED_EARLY
                     if weighed % PAIRS_PER_GROUP == PAIRS_PER_GROUP - 1 and weighed + 1 < PAIRS:

@@ -27,7 +27,7 @@ ALPHA = 1.1
 ENTMAX_EPS = 1e-5
 LN_EPS = 1e-5
 LOGIT_BLOCK = 32
-X_LOAD_GROUPS = 2
+X_LOAD_GROUPS = 3
 UNITS = GROUPS * HALVES
 PRODUCTS = 2 * MASKS
 PAIRS = UNITS * MASKS
@@ -43,7 +43,7 @@ ADDED_LATE = 22
 STORED_LATE = 3
 STORE_PAIR = 2
 VECTOR_PASS = 2
-LN_VECTORS_SLOT = -16
+LN_VECTORS_SLOT = -8
 LAST_PASS = SLOTS * (UNITS - 1)
 EARLY_PASSES = 2
 
@@ -66,7 +66,7 @@ def tile_dynamicfeaturegroupinglayer_e_kernel(
         small = ctx.enter_context(tc.tile_pool(name="small", bufs=4))
         norm_pool = ctx.enter_context(tc.tile_pool(name="norm_pool", bufs=3))
         act_pool = ctx.enter_context(tc.tile_pool(name="act_pool", bufs=3))
-        out_pool = ctx.enter_context(tc.tile_pool(name="out_pool", bufs=2))
+        out_pool = ctx.enter_context(tc.tile_pool(name="out_pool", bufs=4))
         psum_x = ctx.enter_context(tc.psum_pool(name="psum_x", bufs=1))
         psum_measure = ctx.enter_context(tc.psum_pool(name="psum_measure", bufs=2))
         psum_scalar = ctx.enter_context(tc.psum_pool(name="psum_scalar", bufs=4))
@@ -86,13 +86,13 @@ def tile_dynamicfeaturegroupinglayer_e_kernel(
         nc.vector.memset(warm[:], 0.0)
         nc.scalar.activation(out=warm[:], in_=warm[:], func=ACT.Exp)
         nc.vector.memset(zero[:], 0.0)
-        nc.vector.memset(w_planes[:].bitcast(I32), 0)
+        nc.vector.memset(w_planes[:, :, 0, :].bitcast(I32), 0)
         make_identity(nc, identity[:])
         nc.gpsimd.memset(ln_raw[:], 0.0)
         nc.gpsimd.memset(minus_half[:], -0.5)
 
-        def load_x(first_group):
-            cols = slice(first_group * FEATURES, (first_group + X_LOAD_GROUPS) * FEATURES)
+        def load_x(first_group, groups):
+            cols = slice(first_group * FEATURES, (first_group + groups) * FEATURES)
             for h in range(HALVES):
                 nc.sync.dma_start(out=x_rows[h][:, cols], in_=x[h * P : (h + 1) * P, cols])
 
@@ -103,6 +103,17 @@ def tile_dynamicfeaturegroupinglayer_e_kernel(
                     in_=weight_words[w][g].rearrange("p n t -> p (n t)").bitcast(I32),
                 )
 
+        def load_weight_scales(first_group, groups):
+            some = slice(first_group, first_group + groups)
+            for w in range(2):
+                for quadrant in range(4):
+                    nc.sync.dma_start(
+                        out=w_planes[32 * quadrant : 32 * quadrant + 4, w, some, :].bitcast(I32),
+                        in_=weight_scales[w][some, 4 * quadrant : 4 * quadrant + 4, :]
+                        .rearrange("g r n -> r g n")
+                        .bitcast(I32),
+                    )
+
         logit_rows = W_masks.rearrange("g m s -> (g m) s")
         for block in range(P // LOGIT_BLOCK):
             first_row = (mask_rows - LOGIT_BLOCK) * (1 - block % 2)
@@ -110,24 +121,20 @@ def tile_dynamicfeaturegroupinglayer_e_kernel(
                 out=logits[LOGIT_BLOCK * block : LOGIT_BLOCK * (block + 1), :],
                 in_=logit_rows[first_row : first_row + LOGIT_BLOCK, :],
             )
-        load_x(0)
-        for w in range(2):
-            for quadrant in range(4):
-                nc.sync.dma_start(
-                    out=w_planes[32 * quadrant : 32 * quadrant + 4, w, :, :].bitcast(I32),
-                    in_=weight_scales[w][:, 4 * quadrant : 4 * quadrant + 4, :]
-                    .rearrange("g r n -> r g n")
-                    .bitcast(I32),
-                )
+        load_x(0, 1)
+        load_weight_scales(0, 1)
         load_weight_words(0)
         for i, vector in enumerate((ln1_w, ln1_b, ln2_w, ln2_b)):
             nc.sync.dma_start(
                 out=ln_raw[0:ln_rows, i, :], in_=vector.rearrange("g (c j) -> (g c) j", j=P)
             )
-        for g in range(X_LOAD_GROUPS, GROUPS, X_LOAD_GROUPS):
-            load_x(g)
-        for g in range(1, GROUPS):
-            load_weight_words(g)
+
+        def load_the_rest():
+            load_weight_scales(1, GROUPS - 1)
+            for g in range(1, GROUPS, X_LOAD_GROUPS):
+                load_x(g, X_LOAD_GROUPS)
+            for g in range(1, GROUPS):
+                load_weight_words(g)
 
         mask_pt = keep.tile([P, mask_rows, PACK], F32)
         ln_f32 = keep.tile([P, 4, P], F32)
@@ -189,16 +196,18 @@ def tile_dynamicfeaturegroupinglayer_e_kernel(
                 op=ALU.mult,
             )
 
-        def quantise(u):
-            words = code_pool.tile([P, MASKS * P], U32, align_bytes=64)
-            planes = code_pool.tile([P, MASKS * P], U8, align_bytes=64)
+        def quantise(u, masks=range(MASKS)):
+            if 0 in masks:
+                words = code_pool.tile([P, MASKS * P], U32, align_bytes=64)
+                planes = code_pool.tile([P, MASKS * P], U8, align_bytes=64)
+                a_words[u] = words
+                a_planes[u] = planes
+            columns = slice(P * masks[0], P * (masks[-1] + 1))
             nc.vector.quantize_mx(
-                out=words[:].bitcast(FP8X4),
-                scales=planes[:],
-                in_=weighted[u][:].rearrange("p m b t -> p (m b t)"),
+                out=a_words[u][:, columns].bitcast(FP8X4),
+                scales=a_planes[u][:, columns],
+                in_=weighted[u][:, masks[0] : masks[-1] + 1].rearrange("p m b t -> p (m b t)"),
             )
-            a_words[u] = words
-            a_planes[u] = planes
 
         def project(i, pool):
             u, m, w = i // PRODUCTS, i // 2 % MASKS, i % 2
@@ -364,14 +373,15 @@ def tile_dynamicfeaturegroupinglayer_e_kernel(
             )
 
         def make_masks():
+            minus_inverse_alpha = keep.tile([P, 1], F32)
+            nc.vector.tensor_scalar_add(out=minus_inverse_alpha[:], in0=zero[:], scalar1=-1.0 / ALPHA)
             top = keep.tile([P, 1], F32)
             nc.vector.reduce_max(out=top[:], in_=logits[:], axis=AXIS.X)
             minus_alpha_top = keep.tile([P, 1], F32)
             nc.vector.tensor_scalar_mul(out=minus_alpha_top[:], in0=top[:], scalar1=-ALPHA)
             minus_top = keep.tile([P, 1], F32)
             nc.vector.tensor_scalar_mul(out=minus_top[:], in0=top[:], scalar1=-1.0)
-            minus_inverse_alpha = keep.tile([P, 1], F32)
-            nc.vector.tensor_scalar_add(out=minus_inverse_alpha[:], in0=zero[:], scalar1=-1.0 / ALPHA)
+            nc.vector.memset(w_planes[:, :, 1:GROUPS, :].bitcast(I32), 0)
             powered = keep.tile([P, FEATURES], F32)
             total = keep.tile([P, 1], F32)
             nc.scalar.activation(
@@ -393,15 +403,19 @@ def tile_dynamicfeaturegroupinglayer_e_kernel(
             nc.gpsimd.tensor_tensor(
                 out=shrink[:], in0=total_eps[:], in1=minus_inverse_alpha[:], op=ALU.pow
             )
-            mask_rows_tp = keep.tile([P, PACK, P], F32)
-            nc.vector.tensor_scalar_mul(out=mask_rows_tp[:], in0=e_rows_tp[:], scalar1=shrink[:])
-            mask_ps = psum_scalar.tile([P, PACK, P], F32, tag="h")
+            e_ps = psum_scalar.tile([P, PACK, P], F32, tag="h")
             for t in range(PACK):
-                nc.tensor.transpose(
-                    out=mask_ps[:, t, :], in_=mask_rows_tp[:, t, :], identity=identity[:]
-                )
-            nc.vector.tensor_copy(
-                out=mask_pt[:], in_=mask_ps[:, :, 0:mask_rows].rearrange("p t r -> p r t")
+                nc.tensor.transpose(out=e_ps[:, t, :], in_=e_rows_tp[:, t, :], identity=identity[:])
+            shrink_ps = psum_scalar.tile([P, P], F32, tag="h")
+            nc.tensor.matmul(
+                out=shrink_ps[:], lhsT=shrink[:].to_broadcast([P, P]), rhs=identity[:],
+                is_transpose=True, start=True, stop=True,
+            )
+            shrink_row = keep.tile([P, mask_rows], F32)
+            nc.vector.tensor_copy(out=shrink_row[:], in_=shrink_ps[:, 0:mask_rows])
+            nc.vector.tensor_tensor(
+                out=mask_pt[:], in0=e_ps[:, :, 0:mask_rows].rearrange("p t r -> p r t"),
+                in1=shrink_row[:].unsqueeze(2).to_broadcast([P, mask_rows, PACK]), op=ALU.mult,
             )
 
         def widen_layer_norm_vectors():
@@ -454,8 +468,10 @@ def tile_dynamicfeaturegroupinglayer_e_kernel(
         with tc.manual_schedule():
             transpose_x(0)
             make_masks()
-            split_x(1, X_LOAD_GROUPS - 1)
+            load_the_rest()
             widen_layer_norm_vectors()
+            for g in range(1, GROUPS, X_LOAD_GROUPS):
+                split_x(g, X_LOAD_GROUPS)
             for s in range(min(pair_at), LAST_PASS + ADDED_LATE + SLOTS):
                 k = pair_at.get(s)
                 before = pair_at.get(s - 1)
@@ -464,8 +480,6 @@ def tile_dynamicfeaturegroupinglayer_e_kernel(
 
                 if s == LN_VECTORS_SLOT:
                     transpose_layer_norm_vectors()
-                    for g in range(X_LOAD_GROUPS, GROUPS, X_LOAD_GROUPS):
-                        split_x(g, X_LOAD_GROUPS)
                 if weighed_at is not None:
                     weighed = weighed_at + WEIGHED_EARLY
                     if weighed % PAIRS_PER_GROUP == PAIRS_PER_GROUP - 1 and weighed + 1 < PAIRS:
@@ -482,6 +496,8 @@ def tile_dynamicfeaturegroupinglayer_e_kernel(
                 if k is not None:
                     if k + WEIGHED_EARLY < PAIRS:
                         weigh(k + WEIGHED_EARLY)
+                    if -MASKS < k < 0:
+                        quantise(0, [k + MASKS - 1])
                     if k % MASKS == 0 and k > 0:
                         deviations(k // MASKS - 1)
                         scale_and_bias(k // MASKS - 1)
@@ -494,7 +510,9 @@ def tile_dynamicfeaturegroupinglayer_e_kernel(
                         measure(2 * before + 1, measured_ps[2 * before + 1])
                     if before % MASKS == MASKS - 1:
                         u = before // MASKS
-                        if u + 1 < UNITS:
+                        if u == -1:
+                            quantise(0, [MASKS - 1])
+                        elif u + 1 < UNITS:
                             quantise(u + 1)
                         if u >= 0:
                             add_up(u)

@@ -35,14 +35,14 @@ PAIRS_PER_GROUP = HALVES * MASKS
 
 SLOTS = PRODUCTS + 2 * CHUNKS
 PAIR_SLOTS = SLOTS // MASKS
-MEASURED_EARLY = 22
-PAIR_SHIFT = (0, -1, -2, -1)
+MEASURED_EARLY = 21
+FIRST_PAIR_LATE = 1
 X_LATE = 3
 WEIGHED_EARLY = MASKS
-ADDED_LATE = 22
+ADDED_AT = tuple(23 + 2 * c + 2 * (c // 2) for c in range(CHUNKS))
 STORED_LATE = 3
 STORE_PAIR = 2
-VECTOR_PASS = 2
+VECTOR_PASS = 3
 LN_VECTORS_SLOT = -8
 LAST_PASS = SLOTS * (UNITS - 1)
 EARLY_PASSES = 2
@@ -462,9 +462,10 @@ def tile_dynamicfeaturegroupinglayer_e_kernel(
                     multiply(q)
 
         pair_at = {
-            PAIR_SLOTS * k - MEASURED_EARLY + PAIR_SHIFT[k % MASKS]: k
+            PAIR_SLOTS * k - MEASURED_EARLY - (FIRST_PAIR_LATE if k % MASKS > 0 else 0): k
             for k in range(-WEIGHED_EARLY, PAIRS)
         }
+        chunk_at = {SLOTS * (q // CHUNKS) + ADDED_AT[q % CHUNKS]: q for q in range(CHUNKS * UNITS)}
         with tc.manual_schedule():
             transpose_x(0)
             make_masks()
@@ -472,12 +473,10 @@ def tile_dynamicfeaturegroupinglayer_e_kernel(
             widen_layer_norm_vectors()
             for g in range(1, GROUPS, X_LOAD_GROUPS):
                 split_x(g, X_LOAD_GROUPS)
-            for s in range(min(pair_at), LAST_PASS + ADDED_LATE + SLOTS):
+            for s in range(min(pair_at), max(chunk_at) + 2):
                 k = pair_at.get(s)
                 before = pair_at.get(s - 1)
                 weighed_at = pair_at.get(s - X_LATE)
-                added = s - ADDED_LATE
-
                 if s == LN_VECTORS_SLOT:
                     transpose_layer_norm_vectors()
                 if weighed_at is not None:
@@ -490,8 +489,8 @@ def tile_dynamicfeaturegroupinglayer_e_kernel(
                 if 0 <= s < SLOTS * UNITS:
                     for t in passes(s):
                         feed(t)
-                if added > 0 and added % 2 == 1 and added % SLOTS < 2 * CHUNKS and added // SLOTS < UNITS:
-                    add_masks(CHUNKS * (added // SLOTS) + added % SLOTS // 2)
+                if s in chunk_at:
+                    add_masks(chunk_at[s])
 
                 if k is not None:
                     if k + WEIGHED_EARLY < PAIRS:
@@ -519,11 +518,10 @@ def tile_dynamicfeaturegroupinglayer_e_kernel(
                         if u == UNITS - 1:
                             deviations(u)
                             scale_and_bias(u)
-                u = added // SLOTS
-                if s > max(pair_at) and UNITS > u >= UNITS - STORED_LATE:
-                    for c in range(0, CHUNKS, chunks_together(u)):
-                        if added % SLOTS == 2 * (c + chunks_together(u)):
-                            store(CHUNKS * u + c)
+                if s > max(pair_at) and s - 1 in chunk_at:
+                    together = chunks_together(chunk_at[s - 1] // CHUNKS)
+                    if (chunk_at[s - 1] + 1) % together == 0:
+                        store(chunk_at[s - 1] + 1 - together)
                 if 0 <= s < SLOTS * UNITS:
                     for t in passes(s):
                         take(t)

@@ -74,8 +74,8 @@ def tile_dynamicfeaturegroupinglayer_e_kernel(
 
         logits = keep.tile([P, FEATURES], BF16)
         ln_raw = keep.tile([P, 4, P], BF16)
-        w_planes = keep.tile([P, 2, GROUPS, OUTPUTS], U8, align_bytes=64)
-        w_words = keep.tile([P, 2, GROUPS, OUTPUTS], U32, align_bytes=64)
+        w_planes = keep.tile([P, 2, GROUPS, OUTPUTS], U8, align_bytes=256)
+        w_words = keep.tile([P, 2, GROUPS, OUTPUTS], U32, align_bytes=256)
         x_rows = [keep.tile([P, GROUPS * FEATURES], BF16, name="x_rows%d" % h) for h in range(HALVES)]
         x_split = [keep.tile([P, GROUPS, 2, P], F32, name="x_split%d" % h) for h in range(HALVES)]
         minus_half = keep.tile([P, 2 * MASKS], F32)
@@ -198,8 +198,8 @@ def tile_dynamicfeaturegroupinglayer_e_kernel(
 
         def quantise(u, masks=range(MASKS)):
             if 0 in masks:
-                words = code_pool.tile([P, MASKS * P], U32, align_bytes=64)
-                planes = code_pool.tile([P, MASKS * P], U8, align_bytes=64)
+                words = code_pool.tile([P, MASKS * P], U32, align_bytes=256)
+                planes = code_pool.tile([P, MASKS * P], U8, align_bytes=256)
                 a_words[u] = words
                 a_planes[u] = planes
             columns = slice(P * masks[0], P * (masks[-1] + 1))

@@ -43,7 +43,8 @@ ADDED_AT = tuple(23 + 2 * c + 2 * (c // 2) for c in range(CHUNKS))
 STORED_LATE = 3
 STORE_PAIR = 2
 VECTOR_PASS = 3
-LN_VECTORS_SLOT = -8
+X_SLOTS = (-20, -19, -17, -16, -13, -12, -9, -8, -4)
+LN_VECTORS_SLOT = -9
 LAST_PASS = SLOTS * (UNITS - 1)
 EARLY_PASSES = 2
 
@@ -77,7 +78,7 @@ def tile_dynamicfeaturegroupinglayer_e_kernel(
         w_planes = keep.tile([P, 2, GROUPS, OUTPUTS], U8, align_bytes=256)
         w_words = keep.tile([P, 2, GROUPS, OUTPUTS], U32, align_bytes=256)
         x_rows = [keep.tile([P, GROUPS * FEATURES], BF16, name="x_rows%d" % h) for h in range(HALVES)]
-        x_split = [keep.tile([P, GROUPS, 2, P], F32, name="x_split%d" % h) for h in range(HALVES)]
+        x_words = keep.tile([P, GROUPS, HALVES, P, 2], F32)
         minus_half = keep.tile([P, 2 * MASKS], F32)
         identity = keep.tile([P, P], F32)
 
@@ -124,6 +125,8 @@ def tile_dynamicfeaturegroupinglayer_e_kernel(
         load_x(0, 1)
         load_weight_scales(0, 1)
         load_weight_words(0)
+        for g in range(1, GROUPS, X_LOAD_GROUPS):
+            load_x(g, X_LOAD_GROUPS)
         for i, vector in enumerate((ln1_w, ln1_b, ln2_w, ln2_b)):
             nc.sync.dma_start(
                 out=ln_raw[0:ln_rows, i, :], in_=vector.rearrange("g (c j) -> (g c) j", j=P)
@@ -131,15 +134,13 @@ def tile_dynamicfeaturegroupinglayer_e_kernel(
 
         def load_the_rest():
             load_weight_scales(1, GROUPS - 1)
-            for g in range(1, GROUPS, X_LOAD_GROUPS):
-                load_x(g, X_LOAD_GROUPS)
             for g in range(1, GROUPS):
                 load_weight_words(g)
 
         mask_pt = keep.tile([P, mask_rows, PACK], F32)
         ln_f32 = keep.tile([P, 4, P], F32)
         ln_j = keep.tile([P, 4, ln_rows], F32)
-        x_ps = {}
+        kept = {}
         measured_ps = {}
         stats = {}
         products = {}
@@ -158,25 +159,29 @@ def tile_dynamicfeaturegroupinglayer_e_kernel(
         out_ps = {}
         fed_ps = {}
 
-        def split_x(first, groups):
+        def transpose_x(g, pool, tag):
+            words_ps = pool.tile([P, HALVES, 2, P], F32, tag=tag)
             for h in range(HALVES):
-                cols = slice(first * FEATURES, (first + groups) * FEATURES)
-                nc.scalar.copy(
-                    out=x_split[h][:, first : first + groups],
-                    in_=x_rows[h][:, cols].bitcast(F32).rearrange("b (g p u) -> b g u p", p=P, u=2),
-                )
-
-        def transpose_x(g):
-            words_ps = psum_x.tile([P, HALVES, 2, P], F32)
-            for h in range(HALVES):
+                words_of_x = x_rows[h][:].bitcast(F32)
                 for u in range(2):
-                    words = x_rows[h][:].bitcast(F32)[:, u : FEATURES // 2 : 2]
                     nc.tensor.transpose(
                         out=words_ps[:, h, u, :],
-                        in_=words if g == 0 else x_split[h][:, g, u, :],
+                        in_=words_of_x[:, g * FEATURES // 2 + u : (g + 1) * FEATURES // 2 : 2],
                         identity=identity[:],
                     )
-            x_ps[g] = words_ps
+            return words_ps
+
+        def keep_x(g):
+            words_ps = transpose_x(g, psum_scalar, "h")
+            nc.scalar.copy(out=x_words[:, g], in_=words_ps[:].rearrange("p h u b -> p h b u"))
+
+        def keep_masks():
+            masks_ps = psum_x.tile([P, OUTPUTS], F32, tag="x")
+            nc.tensor.matmul(
+                out=masks_ps[:, 0 : mask_rows * PACK], lhsT=identity[:],
+                rhs=mask_pt[:].rearrange("p r t -> p (r t)"), start=True, stop=True,
+            )
+            kept["masks"] = masks_ps
 
         def mask_column(g, m):
             return (MASKS * g + m + LOGIT_BLOCK) % mask_rows
@@ -186,15 +191,22 @@ def tile_dynamicfeaturegroupinglayer_e_kernel(
             if m == 0:
                 rounded = round_pool.tile([P, MASKS, P, PACK], BF16, align_bytes=64)
                 weighted[k // MASKS] = rounded
-            nc.vector.tensor_tensor(
-                out=weighted[k // MASKS][:, m].rearrange("p b (u e) -> p b u e", e=2),
-                in0=x_ps[g][:].bitcast(BF16)[:, h].rearrange("p u (b e) -> p b u e", e=2),
-                in1=mask_pt[:, mask_column(g, m), :]
-                .rearrange("p (u e) -> p u e", e=2)
-                .unsqueeze(1)
-                .to_broadcast([P, P, 2, 2]),
-                op=ALU.mult,
-            )
+            column = mask_column(g, m)
+            if g == 0:
+                in0 = kept["x"][:].bitcast(BF16)[:, h].rearrange("p u (b e) -> p b u e", e=2)
+                in1 = mask_pt[:, column, :].rearrange("p (u e) -> p u e", e=2)
+                in1 = in1.unsqueeze(1).to_broadcast([P, P, 2, 2])
+                result = weighted[k // MASKS][:, m]
+                nc.vector.tensor_tensor(
+                    out=result.rearrange("p b (u e) -> p b u e", e=2), in0=in0, in1=in1, op=ALU.mult
+                )
+            else:
+                in1 = kept["masks"][:, PACK * column : PACK * (column + 1)]
+                nc.vector.tensor_tensor(
+                    out=weighted[k // MASKS][:, m],
+                    in0=x_words[:, g, h].rearrange("p b u -> p (b u)").bitcast(BF16).rearrange("p (b t) -> p b t", t=PACK),
+                    in1=in1.unsqueeze(1).to_broadcast([P, P, PACK]), op=ALU.mult,
+                )
 
         def quantise(u, masks=range(MASKS)):
             if 0 in masks:
@@ -465,24 +477,25 @@ def tile_dynamicfeaturegroupinglayer_e_kernel(
             PAIR_SLOTS * k - MEASURED_EARLY - (FIRST_PAIR_LATE if k % MASKS > 0 else 0): k
             for k in range(-WEIGHED_EARLY, PAIRS)
         }
+        x_at = {X_SLOTS[g - 1]: g for g in range(1, GROUPS)}
         chunk_at = {SLOTS * (q // CHUNKS) + ADDED_AT[q % CHUNKS]: q for q in range(CHUNKS * UNITS)}
         with tc.manual_schedule():
-            transpose_x(0)
+            kept["x"] = transpose_x(0, psum_x, "x")
             make_masks()
             load_the_rest()
             widen_layer_norm_vectors()
-            for g in range(1, GROUPS, X_LOAD_GROUPS):
-                split_x(g, X_LOAD_GROUPS)
             for s in range(min(pair_at), max(chunk_at) + 2):
                 k = pair_at.get(s)
                 before = pair_at.get(s - 1)
                 weighed_at = pair_at.get(s - X_LATE)
+                if s in x_at:
+                    keep_x(x_at[s])
                 if s == LN_VECTORS_SLOT:
                     transpose_layer_norm_vectors()
                 if weighed_at is not None:
                     weighed = weighed_at + WEIGHED_EARLY
-                    if weighed % PAIRS_PER_GROUP == PAIRS_PER_GROUP - 1 and weighed + 1 < PAIRS:
-                        transpose_x((weighed + 1) // PAIRS_PER_GROUP)
+                    if weighed == PAIRS_PER_GROUP - 1:
+                        keep_masks()
                 if k is not None and k >= 0:
                     for i in (2 * k, 2 * k + 1):
                         measured_ps[i] = project(i, psum_measure)

@@ -43,7 +43,8 @@ ADDED_AT = tuple(23 + 2 * c + 2 * (c // 2) for c in range(CHUNKS))
 STORED_LATE = 3
 STORE_PAIR = 2
 VECTOR_PASS = 3
-X_SLOTS = (-20, -19, -17, -16, -13, -12, -9, -8, -4)
+FIRST_X_SLOT = -19
+X_SLOTS = 2
 LN_VECTORS_SLOT = -9
 LAST_PASS = SLOTS * (UNITS - 1)
 EARLY_PASSES = 2
@@ -375,7 +376,7 @@ def tile_dynamicfeaturegroupinglayer_e_kernel(
             width = chunks_together(u) * P
             g, h = u // HALVES, u % HALVES
             out_rows = out_pool.tile([P, OUTPUTS], F32)
-            if u < UNITS - 1:
+            if u < UNITS - 2:
                 nc.vector.tensor_copy(out=out_rows[:, 0:width], in_=out_ps[q][:, 0:width])
             else:
                 nc.scalar.copy(out=out_rows[:, 0:width], in_=out_ps[q][:, 0:width])
@@ -467,7 +468,7 @@ def tile_dynamicfeaturegroupinglayer_e_kernel(
             u, i, q, w = task(s)
             last = u == UNITS - 1
             if q is None:
-                normalise(i, fed_ps[s], w == 0 or s % 4 >= 2 if last else s % SLOTS == VECTOR_PASS)
+                normalise(i, fed_ps[s], w == 0 or s % 2 == 1 if last else s % SLOTS == VECTOR_PASS)
             else:
                 activate(q, w, fed_ps[s], last and w == 1 and q % 2 == 0)
                 if w == 1:
@@ -477,7 +478,7 @@ def tile_dynamicfeaturegroupinglayer_e_kernel(
             PAIR_SLOTS * k - MEASURED_EARLY - (FIRST_PAIR_LATE if k % MASKS > 0 else 0): k
             for k in range(-WEIGHED_EARLY, PAIRS)
         }
-        x_at = {X_SLOTS[g - 1]: g for g in range(1, GROUPS)}
+        x_at = {FIRST_X_SLOT + X_SLOTS * (g - 1): g for g in range(1, GROUPS)}
         chunk_at = {SLOTS * (q // CHUNKS) + ADDED_AT[q % CHUNKS]: q for q in range(CHUNKS * UNITS)}
         with tc.manual_schedule():
             kept["x"] = transpose_x(0, psum_x, "x")

import math
from contextlib import ExitStack

import concourse.mybir as mybir
from concourse.masks import make_identity

F32 = mybir.dt.float32
BF16 = mybir.dt.bfloat16
I32 = mybir.dt.int32
U32 = mybir.dt.uint32
U8 = mybir.dt.uint8
FP8X4 = mybir.dt.float8_e4m3fn_x4
ALU = mybir.AluOpType
ACT = mybir.ActivationFunctionType
AXIS = mybir.AxisListType

P = 128
PACK = 4
BATCH = 256
HALVES = BATCH // P
GROUPS = 10
MASKS = 4
FEATURES = 512
OUTPUTS = 512
CHUNKS = OUTPUTS // P
ALPHA = 1.1
ENTMAX_EPS = 1e-5
LN_EPS = 1e-5
LOGIT_BLOCK = 32
X_LOAD_GROUPS = 3
UNITS = GROUPS * HALVES
PRODUCTS = 2 * MASKS
PAIRS = UNITS * MASKS
PAIRS_PER_GROUP = HALVES * MASKS

SLOTS = PRODUCTS + 2 * CHUNKS
PAIR_SLOTS = SLOTS // MASKS
MEASURED_EARLY = 21
FIRST_PAIR_LATE = 1
X_LATE = 3
WEIGHED_EARLY = MASKS
ADDED_AT = tuple(23 + 2 * c + 2 * (c // 2) for c in range(CHUNKS))
STORED_LATE = 3
STORE_PAIR = 2
VECTOR_PASS = 3
FIRST_X_SLOT = -19
X_SLOTS = 2
LN_VECTORS_SLOT = -9
LAST_PASS = SLOTS * (UNITS - 1)
EARLY_PASSES = 2

FLOPS = 2 * 2 * BATCH * GROUPS * MASKS * FEATURES * OUTPUTS


def tile_dynamicfeaturegroupinglayer_e_kernel(
    tc, x, W_masks, W1_words, W1_scales, W2_words, W2_scales, ln1_w, ln1_b, ln2_w, ln2_b, out
):
    nc = tc.nc
    weight_words = (W1_words, W2_words)
    weight_scales = (W1_scales, W2_scales)
    mask_rows = GROUPS * MASKS
    ln_rows = GROUPS * CHUNKS

    with ExitStack() as ctx:
        keep = ctx.enter_context(tc.tile_pool(name="keep", bufs=1))
        round_pool = ctx.enter_context(tc.tile_pool(name="round_pool", bufs=2))
        code_pool = ctx.enter_context(tc.tile_pool(name="code_pool", bufs=4))
        small = ctx.enter_context(tc.tile_pool(name="small", bufs=4))
        norm_pool = ctx.enter_context(tc.tile_pool(name="norm_pool", bufs=3))
        act_pool = ctx.enter_context(tc.tile_pool(name="act_pool", bufs=3))
        out_pool = ctx.enter_context(tc.tile_pool(name="out_pool", bufs=4))
        psum_x = ctx.enter_context(tc.psum_pool(name="psum_x", bufs=1))
        psum_measure = ctx.enter_context(tc.psum_pool(name="psum_measure", bufs=2))
        psum_scalar = ctx.enter_context(tc.psum_pool(name="psum_scalar", bufs=4))
        psum_sum = ctx.enter_context(tc.psum_pool(name="psum_sum", bufs=1))

        logits = keep.tile([P, FEATURES], BF16)
        ln_raw = keep.tile([P, 4, P], BF16)
        w_planes = keep.tile([P, 2, GROUPS, OUTPUTS], U8, align_bytes=256)
        w_words = keep.tile([P, 2, GROUPS, OUTPUTS], U32, align_bytes=256)
        x_rows = [keep.tile([P, GROUPS * FEATURES], BF16, name="x_rows%d" % h) for h in range(HALVES)]
        x_words = keep.tile([P, GROUPS, HALVES, P, 2], F32)
        minus_half = keep.tile([P, 2 * MASKS], F32)
        identity = keep.tile([P, P], F32)

        warm = keep.tile([P, 1], F32)
        zero = keep.tile([P, 1], F32)
        nc.vector.memset(warm[:], 0.0)
        nc.scalar.activation(out=warm[:], in_=warm[:], func=ACT.Exp)
        nc.vector.memset(zero[:], 0.0)
        nc.vector.memset(w_planes[:, :, 0, :].bitcast(I32), 0)
        make_identity(nc, identity[:])
        nc.gpsimd.memset(ln_raw[:], 0.0)
        nc.gpsimd.memset(minus_half[:], -0.5)

        def load_x(first_group, groups):
            cols = slice(first_group * FEATURES, (first_group + groups) * FEATURES)
            for h in range(HALVES):
                nc.sync.dma_start(out=x_rows[h][:, cols], in_=x[h * P : (h + 1) * P, cols])

        def load_weight_words(g):
            for w in range(2):
                nc.sync.dma_start(
                    out=w_words[:, w, g, :].bitcast(I32),
                    in_=weight_words[w][g].rearrange("p n t -> p (n t)").bitcast(I32),
                )

        def load_weight_scales(first_group, groups):
            some = slice(first_group, first_group + groups)
            for w in range(2):
                for quadrant in range(4):
                    nc.sync.dma_start(
                        out=w_planes[32 * quadrant : 32 * quadrant + 4, w, some, :].bitcast(I32),
                        in_=weight_scales[w][some, 4 * quadrant : 4 * quadrant + 4, :]
                        .rearrange("g r n -> r g n")
                        .bitcast(I32),
                    )

        logit_rows = W_masks.rearrange("g m s -> (g m) s")
        for block in range(P // LOGIT_BLOCK):
            first_row = (mask_rows - LOGIT_BLOCK) * (1 - block % 2)
            nc.sync.dma_start(
                out=logits[LOGIT_BLOCK * block : LOGIT_BLOCK * (block + 1), :],
                in_=logit_rows[first_row : first_row + LOGIT_BLOCK, :],
            )
        load_x(0, 1)
        load_weight_scales(0, 1)
        load_weight_words(0)
        for g in range(1, GROUPS, X_LOAD_GROUPS):
            load_x(g, X_LOAD_GROUPS)
        for i, vector in enumerate((ln1_w, ln1_b, ln2_w, ln2_b)):
            nc.sync.dma_start(
                out=ln_raw[0:ln_rows, i, :], in_=vector.rearrange("g (c j) -> (g c) j", j=P)
            )

        def load_the_rest():
            load_weight_scales(1, GROUPS - 1)
            for g in range(1, GROUPS):
                load_weight_words(g)

        mask_pt = keep.tile([P, mask_rows, PACK], F32)
        ln_f32 = keep.tile([P, 4, P], F32)
        ln_j = keep.tile([P, 4, ln_rows], F32)
        kept = {}
        measured_ps = {}
        stats = {}
        products = {}
        weighted = {}
        a_words = {}
        a_planes = {}
        unit_sums = {}
        differences = {}
        minus_means = {}
        totals = {}
        rstd = {}
        minus_mean_rstd = {}
        normed = {}
        gate = {}
        value = {}
        out_ps = {}
        fed_ps = {}

        def transpose_x(g, pool, tag):
            words_ps = pool.tile([P, HALVES, 2, P], F32, tag=tag)
            for h in range(HALVES):
                words_of_x = x_rows[h][:].bitcast(F32)
                for u in range(2):
                    nc.tensor.transpose(
                        out=words_ps[:, h, u, :],
                        in_=words_of_x[:, g * FEATURES // 2 + u : (g + 1) * FEATURES // 2 : 2],
                        identity=identity[:],
                    )
            return words_ps

        def keep_x(g):
            words_ps = transpose_x(g, psum_scalar, "h")
            nc.scalar.copy(out=x_words[:, g], in_=words_ps[:].rearrange("p h u b -> p h b u"))

        def keep_masks():
            masks_ps = psum_x.tile([P, OUTPUTS], F32, tag="x")
            nc.tensor.matmul(
                out=masks_ps[:, 0 : mask_rows * PACK], lhsT=identity[:],
                rhs=mask_pt[:].rearrange("p r t -> p (r t)"), start=True, stop=True,
            )
            kept["masks"] = masks_ps

        def mask_column(g, m):
            return (MASKS * g + m + LOGIT_BLOCK) % mask_rows

        def weigh(k):
            g, h, m = k // PAIRS_PER_GROUP, k // MASKS % HALVES, k % MASKS
            if m == 0:
                rounded = round_pool.tile([P, MASKS, P, PACK], BF16, align_bytes=64)
                weighted[k // MASKS] = rounded
            column = mask_column(g, m)
            if g == 0:
                in0 = kept["x"][:].bitcast(BF16)[:, h].rearrange("p u (b e) -> p b u e", e=2)
                in1 = mask_pt[:, column, :].rearrange("p (u e) -> p u e", e=2)
                in1 = in1.unsqueeze(1).to_broadcast([P, P, 2, 2])
                result = weighted[k // MASKS][:, m]
                nc.vector.tensor_tensor(
                    out=result.rearrange("p b (u e) -> p b u e", e=2), in0=in0, in1=in1, op=ALU.mult
                )
            else:
                in1 = kept["masks"][:, PACK * column : PACK * (column + 1)]
                nc.vector.tensor_tensor(
                    out=weighted[k // MASKS][:, m],
                    in0=x_words[:, g, h].rearrange("p b u -> p (b u)").bitcast(BF16).rearrange("p (b t) -> p b t", t=PACK),
                    in1=in1.unsqueeze(1).to_broadcast([P, P, PACK]), op=ALU.mult,
                )

        def quantise(u, masks=range(MASKS)):
            if 0 in masks:
                words = code_pool.tile([P, MASKS * P], U32, align_bytes=256)
                planes = code_pool.tile([P, MASKS * P], U8, align_bytes=256)
                a_words[u] = words
                a_planes[u] = planes
            columns = slice(P * masks[0], P * (masks[-1] + 1))
            nc.vector.quantize_mx(
                out=a_words[u][:, columns].bitcast(FP8X4),
                scales=a_planes[u][:, columns],
                in_=weighted[u][:, masks[0] : masks[-1] + 1].rearrange("p m b t -> p (m b t)"),
            )

        def project(i, pool):
            u, m, w = i // PRODUCTS, i // 2 % MASKS, i % 2
            rows = slice(m * P, (m + 1) * P)
            h_ps = pool.tile([P, OUTPUTS], F32, tag="h")
            nc.tensor.matmul_mx(
                out=h_ps[:],
                lhsT=a_words[u][:, rows].bitcast(FP8X4),
                lhsT_scale=a_planes[u][:, rows],
                rhs=w_words[:, w, u // HALVES, :].bitcast(FP8X4),
                rhs_scale=w_planes[:, w, u // HALVES, :],
                start=True,
                stop=True,
            )
            return h_ps

        def measure(i, h_ps):
            u = i // PRODUCTS
            if i % PRODUCTS == 0:
                unit_stats = small.tile([P, 2 * MASKS, 2, 3], F32)
                stats[u] = unit_stats
            nc.vector.bn_stats(
                out=stats[u][:, i % PRODUCTS].rearrange("p s f -> p (s f)"), in_=h_ps[:]
            )

        def add_up(u):
            sums = small.tile([P, 2 * MASKS, 2], F32)
            nc.vector.tensor_reduce(
                out=sums[:], in_=stats[u][:].rearrange("p i s f -> p i f s")[:, :, 1:3, :],
                op=ALU.add, axis=AXIS.X,
            )
            difference = small.tile([P, 2 * MASKS], F32)
            nc.vector.tensor_tensor(
                out=difference[:], in0=stats[u][:, :, 0, 1], in1=stats[u][:, :, 1, 1], op=ALU.subtract
            )
            unit_sums[u] = sums
            differences[u] = difference

        def deviations(u):
            between = small.tile([P, 2 * MASKS], F32)
            nc.vector.scalar_tensor_tensor(
                out=between[:], in0=differences[u][:], scalar=OUTPUTS / 4.0, in1=differences[u][:],
                op0=ALU.mult, op1=ALU.mult,
            )
            minus_mean = small.tile([P, 2 * MASKS], F32)
            nc.vector.tensor_scalar_mul(out=minus_mean[:], in0=unit_sums[u][:, :, 0], scalar1=-0.5)
            minus_means[u] = minus_mean
            total = small.tile([P, 2 * MASKS], F32)
            nc.vector.scalar_tensor_tensor(
                out=total[:], in0=unit_sums[u][:, :, 1], scalar=OUTPUTS * LN_EPS, in1=between[:],
                op0=ALU.add, op1=ALU.add,
            )
            totals[u] = total

        def scale_and_bias(u):
            scale = small.tile([P, 2 * MASKS], F32)
            nc.gpsimd.tensor_tensor(out=scale[:], in0=totals[u][:], in1=minus_half[:], op=ALU.pow)
            bias = small.tile([P, 2 * MASKS], F32)
            nc.gpsimd.tensor_tensor(out=bias[:], in0=minus_means[u][:], in1=scale[:], op=ALU.mult)
            rstd[u] = scale
            minus_mean_rstd[u] = bias

        def normalise(i, h_ps, on_vector):
            u, m, w = i // PRODUCTS, i // 2 % MASKS, i % 2
            column = i % PRODUCTS
            if u not in normed:
                unit_normed = norm_pool.tile([P, 2, MASKS, OUTPUTS], F32)
                normed[u] = unit_normed
            scale = rstd[u][:, column : column + 1]
            bias = minus_mean_rstd[u][:, column : column + 1]
            if on_vector:
                nc.vector.tensor_scalar(
                    out=normed[u][:, w, m, :], in0=h_ps[:], scalar1=scale, scalar2=bias,
                    op0=ALU.mult, op1=ALU.add,
                )
            else:
                nc.scalar.activation(
                    out=normed[u][:, w, m, :], in_=h_ps[:], func=ACT.Identity, scale=scale, bias=bias
                )

        def transpose_normed(q, w):
            u, c = q // CHUNKS, q % CHUNKS
            chunk_ps = psum_scalar.tile([P, MASKS, P], F32, tag="h")
            for m in range(MASKS):
                nc.tensor.transpose(
                    out=chunk_ps[:, m, :],
                    in_=normed[u][:, w, m, c * P : (c + 1) * P],
                    identity=identity[:],
                )
            return chunk_ps

        def activate(q, w, chunk_ps, on_vector):
            u, c = q // CHUNKS, q % CHUNKS
            if u not in gate:
                unit_gate = act_pool.tile([P, CHUNKS, MASKS * P], F32)
                unit_value = act_pool.tile([P, CHUNKS, MASKS * P], F32)
                gate[u] = unit_gate
                value[u] = unit_value
            row = CHUNKS * (u // HALVES) + c
            chunk = chunk_ps[:].rearrange("j m b -> j (m b)")
            if on_vector:
                nc.vector.tensor_scalar(
                    out=value[u][:, c, :], in0=chunk,
                    scalar1=ln_j[:, 2, row : row + 1], scalar2=ln_j[:, 3, row : row + 1],
                    op0=ALU.mult, op1=ALU.add,
                )
                return
            nc.scalar.activation(
                out=(gate, value)[w][u][:, c, :], in_=chunk,
                func=(ACT.Sigmoid, ACT.Relu)[w],
                scale=ln_j[:, 2 * w, row : row + 1], bias=ln_j[:, 2 * w + 1, row : row + 1],
            )

        def multiply(q):
            u, c = q // CHUNKS, q % CHUNKS
            if u == UNITS - 1:
                nc.vector.scalar_tensor_tensor(
                    out=value[u][:, c, :], in0=value[u][:, c, :], scalar=0.0, in1=gate[u][:, c, :],
                    op0=ALU.max, op1=ALU.mult,
                )
            elif c % 2 == 1:
                two = slice(c - 1, c + 1)
                nc.gpsimd.tensor_tensor(
                    out=value[u][:, two, :], in0=value[u][:, two, :], in1=gate[u][:, two, :],
                    op=ALU.mult,
                )

        def add_masks(q):
            u, c = q // CHUNKS, q % CHUNKS
            width = chunks_together(u)
            if c % width == 0:
                if u < UNITS - 1:
                    sums_ps = psum_sum.tile([P, OUTPUTS], F32)
                    out_ps[q] = sums_ps
                else:
                    last_sums_ps = psum_measure.tile([P, OUTPUTS], F32, tag="h")
                    out_ps[q] = last_sums_ps
            for m in range(MASKS):
                nc.tensor.matmul(
                    out=out_ps[q - c % width][:, c % width * P : (c % width + 1) * P],
                    lhsT=value[u][:, c, m * P : (m + 1) * P],
                    rhs=identity[:],
                    is_transpose=True,
                    start=(m == 0),
                    stop=(m == MASKS - 1),
                )

        def chunks_together(u):
            return CHUNKS // 2 if u == UNITS - 1 else CHUNKS

        def store(q):
            u, c = q // CHUNKS, q % CHUNKS
            width = chunks_together(u) * P
            g, h = u // HALVES, u % HALVES
            out_rows = out_pool.tile([P, OUTPUTS], F32)
            if u < UNITS - 2:
                nc.vector.tensor_copy(out=out_rows[:, 0:width], in_=out_ps[q][:, 0:width])
            else:
                nc.scalar.copy(out=out_rows[:, 0:width], in_=out_ps[q][:, 0:width])
            column = g * OUTPUTS + c * P
            nc.sync.dma_start(
                out=out[h * P : (h + 1) * P, column : column + width], in_=out_rows[:, 0:width]
            )

        def make_masks():
            minus_inverse_alpha = keep.tile([P, 1], F32)
            nc.vector.tensor_scalar_add(out=minus_inverse_alpha[:], in0=zero[:], scalar1=-1.0 / ALPHA)
            top = keep.tile([P, 1], F32)
            nc.vector.reduce_max(out=top[:], in_=logits[:], axis=AXIS.X)
            minus_alpha_top = keep.tile([P, 1], F32)
            nc.vector.tensor_scalar_mul(out=minus_alpha_top[:], in0=top[:], scalar1=-ALPHA)
            minus_top = keep.tile([P, 1], F32)
            nc.vector.tensor_scalar_mul(out=minus_top[:], in0=top[:], scalar1=-1.0)
            nc.vector.memset(w_planes[:, :, 1:GROUPS, :].bitcast(I32), 0)
            powered = keep.tile([P, FEATURES], F32)
            total = keep.tile([P, 1], F32)
            nc.scalar.activation(
                out=powered[:], in_=logits[:], func=ACT.Exp,
                bias=minus_alpha_top[:], scale=ALPHA, accum_out=total[:],
            )
            e_rows_tp = keep.tile([P, PACK, P], F32)
            nc.scalar.activation(
                out=e_rows_tp[:], in_=logits[:].rearrange("r (p t) -> r t p", t=PACK),
                func=ACT.Exp, bias=minus_top[:], scale=1.0,
            )
            nc.scalar.activation(out=warm[:], in_=warm[:], func=ACT.Sigmoid)
            total_eps = keep.tile([P, 1], F32)
            nc.gpsimd.tensor_scalar(
                out=total_eps[:], in0=total[:], scalar1=1.0, scalar2=ENTMAX_EPS,
                op0=ALU.mult, op1=ALU.add,
            )
            shrink = keep.tile([P, 1], F32)
            nc.gpsimd.tensor_tensor(
                out=shrink[:], in0=total_eps[:], in1=minus_inverse_alpha[:], op=ALU.pow
            )
            e_ps = psum_scalar.tile([P, PACK, P], F32, tag="h")
            for t in range(PACK):
                nc.tensor.transpose(out=e_ps[:, t, :], in_=e_rows_tp[:, t, :], identity=identity[:])
            shrink_ps = psum_scalar.tile([P, P], F32, tag="h")
            nc.tensor.matmul(
                out=shrink_ps[:], lhsT=shrink[:].to_broadcast([P, P]), rhs=identity[:],
                is_transpose=True, start=True, stop=True,
            )
            shrink_row = keep.tile([P, mask_rows], F32)
            nc.vector.tensor_copy(out=shrink_row[:], in_=shrink_ps[:, 0:mask_rows])
            nc.vector.tensor_tensor(
                out=mask_pt[:], in0=e_ps[:, :, 0:mask_rows].rearrange("p t r -> p r t"),
                in1=shrink_row[:].unsqueeze(2).to_broadcast([P, mask_rows, PACK]), op=ALU.mult,
            )

        def widen_layer_norm_vectors():
            nc.scalar.copy(out=ln_f32[:], in_=ln_raw[:])

        def transpose_layer_norm_vectors():
            ln_ps = psum_scalar.tile([P, 4, P], F32, tag="h")
            for i in range(4):
                nc.tensor.transpose(out=ln_ps[:, i, :], in_=ln_f32[:, i, :], identity=identity[:])
            for i in range(4):
                nc.scalar.activation(
                    out=ln_j[:, i, :], in_=ln_ps[:, i, 0:ln_rows], func=ACT.Identity,
                    scale=math.sqrt(OUTPUTS) if i % 2 == 0 else 1.0,
                )

        def task(s):
            u, j = s // SLOTS, s % SLOTS
            if j < PRODUCTS:
                return u, PRODUCTS * u + 2 * (j % MASKS) + j // MASKS, None, j // MASKS
            return u, None, CHUNKS * u + 2 * ((j - PRODUCTS) // 4) + j % 2, j // 2 % 2

        def passes(s):
            if LAST_PASS - PRODUCTS <= s < LAST_PASS - PRODUCTS + EARLY_PASSES:
                return [s, s + PRODUCTS]
            if LAST_PASS <= s < LAST_PASS + EARLY_PASSES:
                return []
            return [s]

        def feed(s):
            u, i, q, w = task(s)
            if q is not None:
                fed_ps[s] = transpose_normed(q, w)
            else:
                fed_ps[s] = project(i, psum_measure if u == UNITS - 1 and w == 0 else psum_scalar)

        def take(s):
            u, i, q, w = task(s)
            last = u == UNITS - 1
            if q is None:
                normalise(i, fed_ps[s], w == 0 or s % 2 == 1 if last else s % SLOTS == VECTOR_PASS)
            else:
                activate(q, w, fed_ps[s], last and w == 1 and q % 2 == 0)
                if w == 1:
                    multiply(q)

        pair_at = {
            PAIR_SLOTS * k - MEASURED_EARLY - (FIRST_PAIR_LATE if k % MASKS > 0 else 0): k
            for k in range(-WEIGHED_EARLY, PAIRS)
        }
        x_at = {FIRST_X_SLOT + X_SLOTS * (g - 1): g for g in range(1, GROUPS)}
        chunk_at = {SLOTS * (q // CHUNKS) + ADDED_AT[q % CHUNKS]: q for q in range(CHUNKS * UNITS)}
        with tc.manual_schedule():
            kept["x"] = transpose_x(0, psum_x, "x")
            make_masks()
            load_the_rest()
            widen_layer_norm_vectors()
            for s in range(min(pair_at), max(chunk_at) + 2):
                k = pair_at.get(s)
                before = pair_at.get(s - 1)
                weighed_at = pair_at.get(s - X_LATE)
                if s in x_at:
                    keep_x(x_at[s])
                if s == LN_VECTORS_SLOT:
                    transpose_layer_norm_vectors()
                if weighed_at is not None:
                    weighed = weighed_at + WEIGHED_EARLY
                    if weighed == PAIRS_PER_GROUP - 1:
                        keep_masks()
                if k is not None and k >= 0:
                    for i in (2 * k, 2 * k + 1):
                        measured_ps[i] = project(i, psum_measure)
                if 0 <= s < SLOTS * UNITS:
                    for t in passes(s):
                        feed(t)
                if s in chunk_at:
                    add_masks(chunk_at[s])

                if k is not None:
                    if k + WEIGHED_EARLY < PAIRS:
                        weigh(k + WEIGHED_EARLY)
                    if -MASKS < k < 0:
                        quantise(0, [k + MASKS - 1])
                    if k % MASKS == 0 and k > 0:
                        deviations(k // MASKS - 1)
                        scale_and_bias(k // MASKS - 1)
                    if k % MASKS == STORE_PAIR and k // MASKS >= STORED_LATE:
                        store(CHUNKS * (k // MASKS - STORED_LATE))
                    if k >= 0:
                        measure(2 * k, measured_ps[2 * k])
                if before is not None:
                    if before >= 0:
                        measure(2 * before + 1, measured_ps[2 * before + 1])
                    if before % MASKS == MASKS - 1:
                        u = before // MASKS
                        if u == -1:
                            quantise(0, [MASKS - 1])
                        elif u + 1 < UNITS:
                            quantise(u + 1)
                        if u >= 0:
                            add_up(u)
                        if u == UNITS - 1:
                            deviations(u)
                            scale_and_bias(u)
                if s > max(pair_at) and s - 1 in chunk_at:
                    together = chunks_together(chunk_at[s - 1] // CHUNKS)
                    if (chunk_at[s - 1] + 1) % together == 0:
                        store(chunk_at[s - 1] + 1 - together)
                if 0 <= s < SLOTS * UNITS:
                    for t in passes(s):
                        take(t)
